import numpy as np
import ml_dtypes


def mxq(x, axis, fmt="e4m3"):
    dtype, down = {"e4m3": (ml_dtypes.float8_e4m3fn, 7), "e5m2": (ml_dtypes.float8_e5m2, 14)}[fmt]
    v = np.moveaxis(np.asarray(x, np.float32).astype(ml_dtypes.bfloat16).astype(np.float64), axis, -1)
    blocks = v.reshape(v.shape[:-1] + (-1, 32))
    amax = np.abs(blocks).max(-1, keepdims=True)
    byte = np.maximum(np.where(amax > 0, np.frexp(amax)[1] - 1 + 127, 0) - down, 1)
    scale = np.exp2(byte - 127.0)
    codes = (blocks / scale).astype(np.float32).astype(dtype).astype(np.float64)
    return np.moveaxis((codes * scale).reshape(v.shape), -1, axis)


WIDE = False


def mx_kscale(k):
    if not WIDE:
        return np.ones(k)
    levels = np.array([10, -10, 5, -5, 0])
    if k % 512:
        return np.exp2(np.random.permutation(np.resize(levels, k // 32))).repeat(32)
    a = np.empty((k // 512, 16))
    for p in range(k // 512):
        a[p, :8] = np.random.permutation(np.resize(levels, 8))
        for g in range(8):
            far = levels[np.abs(levels - a[p, g]) >= 10]
            a[p, g + 8] = far[np.random.randint(len(far))]
    return np.exp2(a.ravel()).repeat(32)


BF16 = ml_dtypes.bfloat16


def bf(x):
    return np.asarray(x, np.float32).astype(BF16)


def f64(x):
    return np.asarray(x).astype(np.float64)


B, SD, A, H, HS, M, C, F1, F2 = 1024, 896, 128, 1024, 32, 896, 2, 2048, 300
K2 = M + A
EPS = 1e-12


def l2norm(v):
    n = np.sqrt(np.sum(v * v, axis=-1, keepdims=True))
    return v / np.maximum(n, EPS)


def setup_inputs():
    s = mx_kscale(H)
    t = mx_kscale(K2)[M:]
    col = np.concatenate([np.full(M, 0.7), 0.7 / np.sqrt(A) / t])
    return {"xum": bf(np.tanh(np.random.standard_normal((B, H))) * s),
            "action": bf(np.random.standard_normal((B, A)) * t),
            "up_w3": bf(np.random.standard_normal((M, H)) * 1.5 / np.sqrt(H) / s[None, :]),
            "up_b3": bf(np.random.standard_normal(M) * 0.3),
            "dyn_w1_mu": bf(np.random.standard_normal((F1, K2)) * col[None, :]),
            "dyn_b1": bf(np.random.standard_normal(F1) * 0.3)}


def reference(xum, action, up_w3, up_b3, dyn_w1_mu, dyn_b1):
    msg_up = l2norm((mxq(f64(xum), 1, "e4m3") @ mxq(f64(up_w3), 1, "e4m3").T) + f64(up_b3))
    mu = np.concatenate([msg_up, f64(action)], axis=-1)
    return np.maximum((mxq(mu, 1, "e4m3") @ mxq(f64(dyn_w1_mu), 1, "e4m3").T) + f64(dyn_b1), 0.0)

@@ -1,0 +1,322 @@
+import math
+from contextlib import ExitStack
+
+import concourse.mybir as mybir
+from concourse.masks import make_identity
+
+F32 = mybir.dt.float32
+BF16 = mybir.dt.bfloat16
+U32 = mybir.dt.uint32
+U8 = mybir.dt.uint8
+I32 = mybir.dt.int32
+FP8X4 = mybir.dt.float8_e4m3fn_x4
+ACT = mybir.ActivationFunctionType
+ALU = mybir.AluOpType
+
+P = 128
+PACK = 4
+PAIRS = 2
+K = 1024
+PASSES = K // (P * PACK)
+BANK = 512
+
+BATCH = 1024
+MESSAGE = 896
+ACTION = K - MESSAGE
+OUT = 2048
+EPS = 1e-12
+
+B_TILES = BATCH // P
+GROUP = BANK // P
+W1_GROUPS = OUT // BANK
+W3_GROUP_TILES = (4, 2, 1)
+W3_GROUP_START = (0, 512, 768)
+
+ROWS_APART = "(j r) k -> r j k"
+ROWS_TOGETHER = "(r j) k -> r j k"
+
+B1_START = 2 * BANK
+BIAS_COLUMNS = B1_START + OUT
+
+WORDS_IN_TURN = "r (j g p u) -> r j g u p"
+
+LAG = W1_GROUPS
+
+FLOPS = 2 * BATCH * K * (MESSAGE + OUT)
+
+
+def load_rows(nc, pool, rows, row_order, name):
+    n_tiles = rows.shape[0] // P
+    rows_sb = pool.tile([P, n_tiles * K], BF16, name=name)
+    nc.sync.dma_start(
+        out=rows_sb[:].rearrange("r (j k) -> r j k", j=n_tiles),
+        in_=rows.rearrange(row_order, r=P),
+    )
+    return rows_sb
+
+
+def new_group(pools, rows_sb, word_order, name):
+    n_rows = rows_sb.shape[1] // K * P
+    grouped = pools["grouped"].tile([P, PASSES * n_rows * PACK], BF16, tag="grouped", align_bytes=64)
+    return {
+        "n_tiles": n_rows // P,
+        "words": rows_sb[:].bitcast(F32).rearrange(word_order, j=n_rows // P, g=PASSES, u=PAIRS, p=P),
+        "grouped": grouped,
+        "grouped_words": grouped[:].bitcast(F32).rearrange("p (g r u) -> p g r u", g=PASSES, u=PAIRS),
+        "codes": pools["operands"].tile([P, PASSES, n_rows], U32, name=name + "_codes", align_bytes=64),
+        "scales": pools["operands"].tile([P, PASSES, n_rows], U8, name=name + "_scales", align_bytes=64),
+    }
+
+
+def flip_row_tile(nc, pools, identity, group, j):
+    flipped = pools["psum"].tile([P, PASSES, PAIRS, P], F32, tag="bank")
+    for g in range(PASSES):
+        for u in range(PAIRS):
+            nc.tensor.transpose(flipped[:, g, u, :], group["words"][:, j, g, u, :], identity[:])
+    copy = nc.vector.tensor_copy if j == 1 else nc.scalar.copy
+    copy(
+        out=group["grouped_words"][:, :, j * P : (j + 1) * P, :],
+        in_=flipped[:].rearrange("p g u r -> p g r u"),
+    )
+
+
+def quantise_group(nc, group):
+    width = group["n_tiles"] * P * PACK
+    for g in range(PASSES):
+        nc.vector.quantize_mx(
+            out=group["codes"][:, g, :].bitcast(FP8X4),
+            scales=group["scales"][:, g, :],
+            in_=group["grouped"][:, g * width : (g + 1) * width],
+        )
+
+
+def tile_modelgraphpolicy_pb_kernel(tc, xum, action, up_w3, up_b3, dyn_w1_mu, dyn_b1, out):
+    nc = tc.nc
+    with ExitStack() as ctx:
+        const = ctx.enter_context(tc.tile_pool(name="const", bufs=1))
+        raw = ctx.enter_context(tc.tile_pool(name="raw", bufs=1))
+        work = ctx.enter_context(tc.tile_pool(name="work", bufs=3))
+        small = ctx.enter_context(tc.tile_pool(name="small", bufs=3))
+        results = ctx.enter_context(tc.tile_pool(name="results", bufs=6))
+        pools = {
+            "operands": ctx.enter_context(tc.tile_pool(name="operands", bufs=1)),
+            "grouped": ctx.enter_context(tc.tile_pool(name="grouped", bufs=3)),
+            "psum": ctx.enter_context(tc.psum_pool(name="psum", bufs=8)),
+        }
+        psum = pools["psum"]
+        ctx.enter_context(tc.manual_schedule())
+
+        bias_rows = const.tile([P, BIAS_COLUMNS], BF16)
+        nc.vector.memset(bias_rows[:].bitcast(I32), 0)
+        nc.scalar.dma_start(out=bias_rows[0:1, 0:MESSAGE], in_=up_b3.unsqueeze(0))
+        nc.scalar.dma_start(out=bias_rows[0:1, B1_START:BIAS_COLUMNS], in_=dyn_b1.unsqueeze(0))
+        x_rows = [load_rows(nc, raw, xum[0:BANK, :], ROWS_TOGETHER, "x_rows0")]
+        w3_rows = [
+            load_rows(nc, raw, up_w3[start : start + tiles * P, :], ROWS_APART, "w3_rows%d" % start)
+            for start, tiles in zip(W3_GROUP_START, W3_GROUP_TILES)
+        ]
+        x_rows.append(load_rows(nc, raw, xum[BANK : 2 * BANK, :], ROWS_TOGETHER, "x_rows1"))
+        action_sb = raw.tile([P, B_TILES, ACTION], BF16)
+        nc.sync.dma_start(
+            out=action_sb[:].rearrange("r (h j) a -> r h j a", j=GROUP),
+            in_=action.rearrange("(h r j) a -> r h j a", r=P, j=GROUP),
+        )
+        w1_rows = [
+            load_rows(nc, raw, dyn_w1_mu[n * BANK : (n + 1) * BANK, :], ROWS_APART, "w1_rows%d" % n)
+            for n in range(W1_GROUPS)
+        ]
+        out_tiles = out.rearrange("(h r j) n -> h j r n", r=P, j=GROUP)
+
+        identity_f32 = const.tile([P, P], F32)
+        make_identity(nc, identity_f32[:])
+        identity_bf16 = const.tile([P, P], BF16)
+        make_identity(nc, identity_bf16[:])
+        one = const.tile([P, 1], F32)
+        nc.vector.memset(one[:], 1.0)
+        nc.scalar.sqrt(one[:], one[:])
+
+        ones = const.tile([P, P], BF16)
+        nc.vector.memset(ones[:], 1.0)
+        bias_all = const.tile([P, BIAS_COLUMNS], BF16)
+
+        def spread_bias(piece):
+            columns = slice(piece * BANK, (piece + 1) * BANK)
+            spread = psum.tile([P, BANK], F32, tag="bank")
+            nc.tensor.matmul(out=spread[:], lhsT=ones[:], rhs=bias_rows[:, columns], start=True, stop=True)
+            nc.scalar.copy(out=bias_all[:, columns], in_=spread[:])
+
+        mu_planes = raw.tile([P, B_TILES, PASSES, PACK, P], BF16)
+        message_p = (MESSAGE - P * PACK) // PACK
+        mu_codes = pools["operands"].tile([P, B_TILES, PASSES, P], U32, align_bytes=64)
+        mu_scales = pools["operands"].tile([P, B_TILES, PASSES, P], U8, align_bytes=64)
+
+        groups = []
+        spread_bias(0)
+        for rows_sb, name in zip([x_rows[0]] + w3_rows + [x_rows[1]], ["x0", "w3_0", "w3_1", "w3_2", "x1"]):
+            group = new_group(pools, rows_sb, WORDS_IN_TURN, name)
+            for j in range(group["n_tiles"]):
+                flip_row_tile(nc, pools, identity_f32, group, j)
+            if groups:
+                quantise_group(nc, groups[-1])
+            groups.append(group)
+            spread_bias(len(groups))
+        x_groups = [groups[0], groups[4]]
+        w3_groups = groups[1:4]
+        w1_groups = []
+
+        z_ps, z, norm, inverse, mu_flipped, mu_grouped = {}, {}, {}, {}, {}, {}
+
+        def first_matmul(i):
+            x = x_groups[i // GROUP]
+            b_cols = slice((i % GROUP) * P, (i % GROUP + 1) * P)
+            z_ps[i] = [psum.tile([P, BANK], F32, tag="bank", name="z_ps%d" % h) for h in range(2)]
+            for w3, start in zip(w3_groups, W3_GROUP_START):
+                width = w3["n_tiles"] * P
+                for g in range(PASSES):
+                    nc.tensor.matmul_mx(
+                        out=z_ps[i][start // BANK][:, start % BANK : start % BANK + width],
+                        lhsT=x["codes"][:, g, b_cols].bitcast(FP8X4),
+                        lhsT_scale=x["scales"][:, g, b_cols],
+                        rhs=w3["codes"][:, g, :].bitcast(FP8X4),
+                        rhs_scale=w3["scales"][:, g, :],
+                        start=(g == 0),
+                        stop=(g == PASSES - 1),
+                    )
+
+        def add_first_bias(i):
+            z[i] = work.tile([P, MESSAGE], F32, tag="z", name="z")
+            nc.vector.tensor_tensor(
+                out=z[i][:, 0:BANK], in0=z_ps[i][0][:], in1=bias_all[:, 0:BANK], op=ALU.add
+            )
+            nc.vector.tensor_tensor(
+                out=z[i][:, BANK:MESSAGE],
+                in0=z_ps[i][1][:, 0 : MESSAGE - BANK],
+                in1=bias_all[:, BANK:MESSAGE],
+                op=ALU.add,
+            )
+
+        def take_norm(i):
+            squares = work.tile([P, MESSAGE], F32, tag="squares")
+            sum_squares = small.tile([P, 1], F32, tag="sum_squares")
+            nc.scalar.activation(out=squares[:], in_=z[i][:], func=ACT.Square, accum_out=sum_squares[:])
+            norm[i] = small.tile([P, 1], F32, tag="norm", name="norm")
+            nc.scalar.sqrt(norm[i][:], sum_squares[:])
+
+        def invert_norm(i):
+            floored = small.tile([P, 1], F32, tag="floored")
+            nc.vector.tensor_scalar_max(floored[:], norm[i][:], EPS)
+            inverse[i] = small.tile([P, 1], F32, tag="inverse", name="inverse")
+            nc.vector.reciprocal(inverse[i][:], floored[:])
+
+        def round_message(i):
+            for g, first, last in ((0, 0, P * PACK), (1, P * PACK, MESSAGE)):
+                planes = mu_planes[:, i, g, :, 0 : (last - first) // PACK].rearrange("b t p -> b p t")
+                columns = z[i][:, first:last].rearrange("b (p t) -> b p t", t=PACK)
+                if i < LAG:
+                    nc.gpsimd.tensor_scalar(
+                        out=planes,
+                        in0=columns,
+                        scalar1=inverse[i][:],
+                        scalar2=0.0,
+                        op0=ALU.mult,
+                        op1=ALU.add,
+                    )
+                else:
+                    nc.scalar.activation(out=planes, in_=columns, func=ACT.Copy, scale=inverse[i][:])
+
+        def flip_mu(i):
+            mu_flipped[i] = psum.tile([P, PASSES, PACK, P], BF16, tag="bank", name="mu_flipped")
+            for g in range(PASSES):
+                for t in range(PACK):
+                    nc.tensor.transpose(
+                        mu_flipped[i][:, g, t, :], mu_planes[:, i, g, t, :], identity_bf16[:]
+                    )
+
+        def group_mu(i):
+            mu_grouped[i] = work.tile(
+                [P, PASSES, P, PACK], BF16, tag="mu_grouped", name="mu_grouped", align_bytes=64
+            )
+            nc.scalar.copy(out=mu_grouped[i][:], in_=mu_flipped[i][:].rearrange("p g t b -> p g b t"))
+
+        def quantise_mu(i):
+            nc.vector.quantize_mx(
+                out=mu_codes[:, i].rearrange("p g b -> p (g b)").bitcast(FP8X4),
+                scales=mu_scales[:, i].rearrange("p g b -> p (g b)"),
+                in_=mu_grouped[i][:].rearrange("p g b t -> p (g b t)"),
+            )
+
+        def link(stage, i):
+            if 0 <= i < B_TILES:
+                stage(i)
+
+        result = {}
+
+        def second_matmul(i, n):
+            w1 = w1_groups[n]
+            acc = psum.tile([P, BANK], F32, tag="bank")
+            for g in range(PASSES):
+                nc.tensor.matmul_mx(
+                    out=acc[:],
+                    lhsT=mu_codes[:, i, g, :].bitcast(FP8X4),
+                    lhsT_scale=mu_scales[:, i, g, :],
+                    rhs=w1["codes"][:, g, :].bitcast(FP8X4),
+                    rhs_scale=w1["scales"][:, g, :],
+                    start=(g == 0),
+                    stop=(g == PASSES - 1),
+                )
+            side = n % 2
+            if side == 0:
+                result[i] = results.tile([P, 2 * BANK], F32, tag="result", name="result")
+            nc.vector.tensor_tensor(
+                out=result[i][:, side * BANK : (side + 1) * BANK],
+                in0=acc[:],
+                in1=bias_all[:, B1_START + n * BANK : B1_START + (n + 1) * BANK],
+                op=ALU.add,
+            )
+            if side == 1:
+                if i < LAG:
+                    nc.gpsimd.tensor_scalar(
+                        out=result[i][:],
+                        in0=result[i][:],
+                        scalar1=math.inf,
+                        scalar2=0.0,
+                        op0=ALU.min,
+                        op1=ALU.max,
+                    )
+                else:
+                    nc.scalar.activation(out=result[i][:], in_=result[i][:], func=ACT.Relu)
+                nc.sync.dma_start(
+                    out=out_tiles[i // GROUP, i % GROUP, :, (n - 1) * BANK : (n + 1) * BANK],
+                    in_=result[i][:],
+                )
+
+        def bulk_quarter(step, quarter):
+            if step <= W1_GROUPS and quarter == 1:
+                quantise_group(nc, groups[-1])
+            if step < W1_GROUPS:
+                if quarter == 0:
+                    w1_groups.append(new_group(pools, w1_rows[step], WORDS_IN_TURN, "w1_%d" % step))
+                flip_row_tile(nc, pools, identity_f32, w1_groups[step], quarter)
+                if quarter == GROUP - 1:
+                    groups.append(w1_groups[step])
+            if step >= LAG:
+                second_matmul(step - LAG, quarter)
+
+        nc.vector.tensor_copy(
+            out=mu_planes[:, :, 1, :, message_p:P],
+            in_=action_sb[:].rearrange("b i (p t) -> b i t p", t=PACK),
+        )
+
+        for step in range(B_TILES + LAG):
+            link(invert_norm, step - 1)
+            link(flip_mu, step - 2)
+            link(first_matmul, step)
+            bulk_quarter(step, 0)
+            link(round_message, step - 1)
+            link(add_first_bias, step)
+            bulk_quarter(step, 1)
+            link(group_mu, step - 2)
+            link(quantise_mu, step - 3)
+            bulk_quarter(step, 2)
+            link(take_norm, step)
+            bulk_quarter(step, 3)

@@ -29,65 +29,13 @@ EPS = 1e-12
 B_TILES = BATCH // P
 GROUP = BANK // P
 W1_GROUPS = OUT // BANK
+W3_TILES = MESSAGE // P
 W3_GROUP_TILES = (4, 2, 1)
-W3_GROUP_START = (0, 512, 768)
+W3_GROUP_START = (0, 4, 6)
 
-ROWS_APART = "(j r) k -> r j k"
-ROWS_TOGETHER = "(r j) k -> r j k"
-
-B1_START = 2 * BANK
-BIAS_COLUMNS = B1_START + OUT
-
-WORDS_IN_TURN = "r (j g p u) -> r j g u p"
-
-LAG = W1_GROUPS
+LAG = 2
 
 FLOPS = 2 * BATCH * K * (MESSAGE + OUT)
-
-
-def load_rows(nc, pool, rows, row_order, name):
-    n_tiles = rows.shape[0] // P
-    rows_sb = pool.tile([P, n_tiles * K], BF16, name=name)
-    nc.sync.dma_start(
-        out=rows_sb[:].rearrange("r (j k) -> r j k", j=n_tiles),
-        in_=rows.rearrange(row_order, r=P),
-    )
-    return rows_sb
-
-
-def new_group(pools, rows_sb, word_order, name):
-    n_rows = rows_sb.shape[1] // K * P
-    grouped = pools["grouped"].tile([P, PASSES * n_rows * PACK], BF16, tag="grouped", align_bytes=64)
-    return {
-        "n_tiles": n_rows // P,
-        "words": rows_sb[:].bitcast(F32).rearrange(word_order, j=n_rows // P, g=PASSES, u=PAIRS, p=P),
-        "grouped": grouped,
-        "grouped_words": grouped[:].bitcast(F32).rearrange("p (g r u) -> p g r u", g=PASSES, u=PAIRS),
-        "codes": pools["operands"].tile([P, PASSES, n_rows], U32, name=name + "_codes", align_bytes=64),
-        "scales": pools["operands"].tile([P, PASSES, n_rows], U8, name=name + "_scales", align_bytes=64),
-    }
-
-
-def flip_row_tile(nc, pools, identity, group, j):
-    flipped = pools["psum"].tile([P, PASSES, PAIRS, P], F32, tag="bank")
-    for g in range(PASSES):
-        for u in range(PAIRS):
-            nc.tensor.transpose(flipped[:, g, u, :], group["words"][:, j, g, u, :], identity[:])
-    copy = nc.vector.tensor_copy if j == 1 else nc.scalar.copy
-    copy(
-        out=group["grouped_words"][:, :, j * P : (j + 1) * P, :],
-        in_=flipped[:].rearrange("p g u r -> p g r u"),
-    )
-
-
-def quantise_group(nc, group):
-    width = group["n_tiles"] * P * PACK
-    for g in range(PASSES):
-        nc.vector.quantize_mx(
-            out=group["codes"][:, g, :].bitcast(FP8X4),
-            scales=group["scales"][:, g, :],
-            in_=group["grouped"][:, g * width : (g + 1) * width],
-        )
 
 
 def tile_modelgraphpolicy_pb_kernel(tc, xum, action, up_w3, up_b3, dyn_w1_mu, dyn_b1, out):
@@ -95,228 +43,327 @@ def tile_modelgraphpolicy_pb_kernel(tc, xum, action, up_w3, up_b3, dyn_w1_mu, dy
     with ExitStack() as ctx:
         const = ctx.enter_context(tc.tile_pool(name="const", bufs=1))
         raw = ctx.enter_context(tc.tile_pool(name="raw", bufs=1))
+        operands = ctx.enter_context(tc.tile_pool(name="operands", bufs=1))
+        grouped_pool = ctx.enter_context(tc.tile_pool(name="grouped", bufs=4))
         work = ctx.enter_context(tc.tile_pool(name="work", bufs=3))
         small = ctx.enter_context(tc.tile_pool(name="small", bufs=3))
         results = ctx.enter_context(tc.tile_pool(name="results", bufs=6))
-        pools = {
-            "operands": ctx.enter_context(tc.tile_pool(name="operands", bufs=1)),
-            "grouped": ctx.enter_context(tc.tile_pool(name="grouped", bufs=3)),
-            "psum": ctx.enter_context(tc.psum_pool(name="psum", bufs=8)),
-        }
-        psum = pools["psum"]
+        psum = ctx.enter_context(tc.psum_pool(name="psum", bufs=8))
         ctx.enter_context(tc.manual_schedule())
 
-        bias_rows = const.tile([P, BIAS_COLUMNS], BF16)
-        nc.vector.memset(bias_rows[:].bitcast(I32), 0)
-        nc.scalar.dma_start(out=bias_rows[0:1, 0:MESSAGE], in_=up_b3.unsqueeze(0))
-        nc.scalar.dma_start(out=bias_rows[0:1, B1_START:BIAS_COLUMNS], in_=dyn_b1.unsqueeze(0))
-        x_rows = [load_rows(nc, raw, xum[0:BANK, :], ROWS_TOGETHER, "x_rows0")]
-        w3_rows = [
-            load_rows(nc, raw, up_w3[start : start + tiles * P, :], ROWS_APART, "w3_rows%d" % start)
-            for start, tiles in zip(W3_GROUP_START, W3_GROUP_TILES)
-        ]
-        x_rows.append(load_rows(nc, raw, xum[BANK : 2 * BANK, :], ROWS_TOGETHER, "x_rows1"))
-        action_sb = raw.tile([P, B_TILES, ACTION], BF16)
-        nc.sync.dma_start(
-            out=action_sb[:].rearrange("r (h j) a -> r h j a", j=GROUP),
-            in_=action.rearrange("(h r j) a -> r h j a", r=P, j=GROUP),
-        )
-        w1_rows = [
-            load_rows(nc, raw, dyn_w1_mu[n * BANK : (n + 1) * BANK, :], ROWS_APART, "w1_rows%d" % n)
-            for n in range(W1_GROUPS)
-        ]
-        out_tiles = out.rearrange("(h r j) n -> h j r n", r=P, j=GROUP)
+        bias1 = const.tile([P, MESSAGE], BF16)
+        bias2 = const.tile([P, OUT], BF16)
+
+        def load_pair(rows, row_order, name):
+            pair = raw.tile([P, 2, K], BF16, name=name)
+            nc.sync.dma_start(out=pair[:], in_=rows.rearrange(row_order, r=P))
+            return pair
+
+        w3_rows = []
+        for j in range(W3_TILES):
+            tile = raw.tile([P, K], BF16, name="w3_rows%d" % j)
+            nc.sync.dma_start(out=tile[:], in_=up_w3[j * P : (j + 1) * P, :])
+            w3_rows.append(tile)
+
+        x_pairs = {}
+        w1_pairs = {}
+        mu = raw.tile([P, B_TILES, K], BF16)
+
+        def load_x(s):
+            x_pairs[s] = load_pair(xum[2 * P * s : 2 * P * (s + 1), :], "(r j) k -> r j k", "x_rows%d" % s)
+
+        def load_w1(n):
+            for s in (2 * n, 2 * n + 1):
+                w1_pairs[s] = load_pair(
+                    dyn_w1_mu[2 * P * s : 2 * P * (s + 1), :], "(j r) k -> r j k", "w1_rows%d" % s
+                )
+
+        load_x(0)
+        nc.sync.dma_start(out=bias1[:], in_=up_b3.partition_broadcast(P))
+        load_w1(0)
+        load_x(1)
+        load_w1(1)
+        for s in range(B_TILES // 2):
+            nc.sync.dma_start(
+                out=mu[:, 2 * s : 2 * s + 2, MESSAGE:K],
+                in_=action[2 * P * s : 2 * P * (s + 1), :].rearrange("(r j) a -> r j a", j=2),
+            )
+        load_w1(2)
+        load_x(2)
+        load_w1(3)
+        nc.sync.dma_start(out=bias2[:], in_=dyn_b1.partition_broadcast(P))
+        load_x(3)
+        out_tiles = out.rearrange("(s r j) n -> s j r n", r=P, j=2)
 
         identity_f32 = const.tile([P, P], F32)
         make_identity(nc, identity_f32[:])
-        identity_bf16 = const.tile([P, P], BF16)
-        make_identity(nc, identity_bf16[:])
         one = const.tile([P, 1], F32)
         nc.vector.memset(one[:], 1.0)
         nc.scalar.sqrt(one[:], one[:])
 
-        ones = const.tile([P, P], BF16)
-        nc.vector.memset(ones[:], 1.0)
-        bias_all = const.tile([P, BIAS_COLUMNS], BF16)
+        def flip(words):
+            flipped = psum.tile([P, PASSES, PAIRS, P], F32, tag="bank", name="flipped")
+            turned = words.rearrange("r (g p u) -> r g u p", g=PASSES, u=PAIRS)
+            for g in range(PASSES):
+                for u in range(PAIRS):
+                    nc.tensor.transpose(flipped[:, g, u, :], turned[:, g, u, :], identity_f32[:])
+            return flipped
 
-        def spread_bias(piece):
-            columns = slice(piece * BANK, (piece + 1) * BANK)
-            spread = psum.tile([P, BANK], F32, tag="bank")
-            nc.tensor.matmul(out=spread[:], lhsT=ones[:], rhs=bias_rows[:, columns], start=True, stop=True)
-            nc.scalar.copy(out=bias_all[:, columns], in_=spread[:])
+        wide_pool = ctx.enter_context(tc.tile_pool(name="wide", bufs=1))
 
-        mu_planes = raw.tile([P, B_TILES, PASSES, PACK, P], BF16)
-        message_p = (MESSAGE - P * PACK) // PACK
-        mu_codes = pools["operands"].tile([P, B_TILES, PASSES, P], U32, align_bytes=64)
-        mu_scales = pools["operands"].tile([P, B_TILES, PASSES, P], U8, align_bytes=64)
+        def new_group(tiles):
+            pool = grouped_pool if tiles < GROUP else wide_pool
+            return pool.tile(
+                [P, PASSES, tiles * P, PACK], BF16, tag="grouped%d" % tiles, name="grouped", align_bytes=64
+            )
 
-        groups = []
-        spread_bias(0)
-        for rows_sb, name in zip([x_rows[0]] + w3_rows + [x_rows[1]], ["x0", "w3_0", "w3_1", "w3_2", "x1"]):
-            group = new_group(pools, rows_sb, WORDS_IN_TURN, name)
-            for j in range(group["n_tiles"]):
-                flip_row_tile(nc, pools, identity_f32, group, j)
-            if groups:
-                quantise_group(nc, groups[-1])
-            groups.append(group)
-            spread_bias(len(groups))
-        x_groups = [groups[0], groups[4]]
-        w3_groups = groups[1:4]
-        w1_groups = []
+        def empty(copy, flipped, grouped, j):
+            copy(
+                out=grouped[:, :, j * P : (j + 1) * P, :].rearrange("p g r t -> p g (r t)").bitcast(F32).rearrange(
+                    "p g (r u) -> p g r u", u=PAIRS
+                ),
+                in_=flipped[:].rearrange("p g u r -> p g r u"),
+            )
 
-        z_ps, z, norm, inverse, mu_flipped, mu_grouped = {}, {}, {}, {}, {}, {}
+        on_scalar = nc.scalar.copy
+        on_vector = nc.vector.tensor_copy
+
+        def quantise(grouped, codes, scales):
+            nc.vector.quantize_mx(
+                out=codes.bitcast(FP8X4), scales=scales, in_=grouped.rearrange("p c t -> p (c t)")
+            )
+
+        def quantise_stationary(grouped, codes, scales):
+            nc.vector.quantize_mx(
+                out=codes.rearrange("p g b -> p (g b)").bitcast(FP8X4),
+                scales=scales.rearrange("p g b -> p (g b)"),
+                in_=grouped[:].rearrange("p g b t -> p (g b t)"),
+            )
+
+        x_codes = operands.tile([P, B_TILES, PASSES, P], U32, align_bytes=64)
+        x_scales = operands.tile([P, B_TILES, PASSES, P], U8, align_bytes=64)
+        mu_codes = operands.tile([P, B_TILES, PASSES, P], U32, align_bytes=64)
+        mu_scales = operands.tile([P, B_TILES, PASSES, P], U8, align_bytes=64)
+        w3_codes = [
+            operands.tile([P, PASSES, n * P], U32, name="w3_codes%d" % n, align_bytes=64) for n in W3_GROUP_TILES
+        ]
+        w3_scales = [
+            operands.tile([P, PASSES, n * P], U8, name="w3_scales%d" % n, align_bytes=64) for n in W3_GROUP_TILES
+        ]
+        w1_codes = [
+            operands.tile([P, PASSES, BANK], U32, name="w1_codes%d" % n, align_bytes=64) for n in range(W1_GROUPS)
+        ]
+        w1_scales = [
+            operands.tile([P, PASSES, BANK], U8, name="w1_scales%d" % n, align_bytes=64) for n in range(W1_GROUPS)
+        ]
+
+        x_flipped, x_grouped, w1_flipped, w1_grouped = {}, {}, {}, {}
+        z_ps, z, norm, floored, inverse, mu_flipped, mu_grouped = {}, {}, {}, {}, {}, {}, {}
+
+        def flip_x(i):
+            if i < B_TILES:
+                x_flipped[i] = flip(x_pairs[i // 2][:, i % 2, :].bitcast(F32))
+
+        def empty_x(i):
+            if i < B_TILES:
+                x_grouped[i] = new_group(1)
+                empty(on_scalar, x_flipped[i], x_grouped[i], 0)
+
+        def quantise_x(i):
+            if i < B_TILES:
+                quantise_stationary(x_grouped[i], x_codes[:, i], x_scales[:, i])
+
+        def flip_w1(j):
+            w1_flipped[j] = flip(w1_pairs[j // 2][:, j % 2, :].bitcast(F32))
+
+        def empty_w1(j, copy):
+            if j % 2 == 0:
+                w1_grouped[j // 2] = new_group(2)
+            empty(copy, w1_flipped[j], w1_grouped[j // 2], j % 2)
+
+        def quantise_w1(s):
+            columns = slice((s % 2) * 2 * P, (s % 2 + 1) * 2 * P)
+            for g in range(PASSES):
+                quantise(
+                    w1_grouped[s][:, g], w1_codes[s // 2][:, g, columns], w1_scales[s // 2][:, g, columns]
+                )
 
         def first_matmul(i):
-            x = x_groups[i // GROUP]
-            b_cols = slice((i % GROUP) * P, (i % GROUP + 1) * P)
             z_ps[i] = [psum.tile([P, BANK], F32, tag="bank", name="z_ps%d" % h) for h in range(2)]
-            for w3, start in zip(w3_groups, W3_GROUP_START):
-                width = w3["n_tiles"] * P
+            for codes, scales, first, tiles in zip(w3_codes, w3_scales, W3_GROUP_START, W3_GROUP_TILES):
+                start, width = first * P, tiles * P
                 for g in range(PASSES):
                     nc.tensor.matmul_mx(
                         out=z_ps[i][start // BANK][:, start % BANK : start % BANK + width],
-                        lhsT=x["codes"][:, g, b_cols].bitcast(FP8X4),
-                        lhsT_scale=x["scales"][:, g, b_cols],
-                        rhs=w3["codes"][:, g, :].bitcast(FP8X4),
-                        rhs_scale=w3["scales"][:, g, :],
+                        lhsT=x_codes[:, i, g, :].bitcast(FP8X4),
+                        lhsT_scale=x_scales[:, i, g, :],
+                        rhs=codes[:, g, :].bitcast(FP8X4),
+                        rhs_scale=scales[:, g, :],
                         start=(g == 0),
                         stop=(g == PASSES - 1),
                     )
 
-        def add_first_bias(i):
+        def add_first_bias(i, between=lambda: None):
             z[i] = work.tile([P, MESSAGE], F32, tag="z", name="z")
-            nc.vector.tensor_tensor(
-                out=z[i][:, 0:BANK], in0=z_ps[i][0][:], in1=bias_all[:, 0:BANK], op=ALU.add
-            )
-            nc.vector.tensor_tensor(
-                out=z[i][:, BANK:MESSAGE],
-                in0=z_ps[i][1][:, 0 : MESSAGE - BANK],
-                in1=bias_all[:, BANK:MESSAGE],
-                op=ALU.add,
-            )
+            for h, first, last in ((0, 0, BANK), (1, BANK, MESSAGE)):
+                if h == 1: between()
+                nc.vector.tensor_tensor(
+                    out=z[i][:, first:last],
+                    in0=z_ps[i][h][:, 0 : last - first],
+                    in1=bias1[:, first:last],
+                    op=ALU.add,
+                )
 
         def take_norm(i):
-            squares = work.tile([P, MESSAGE], F32, tag="squares")
-            sum_squares = small.tile([P, 1], F32, tag="sum_squares")
+            squares = work.tile([P, MESSAGE], F32, tag="squares", name="squares")
+            sum_squares = small.tile([P, 1], F32, tag="sum_squares", name="sum_squares")
             nc.scalar.activation(out=squares[:], in_=z[i][:], func=ACT.Square, accum_out=sum_squares[:])
             norm[i] = small.tile([P, 1], F32, tag="norm", name="norm")
             nc.scalar.sqrt(norm[i][:], sum_squares[:])
 
+        def floor_norm(i):
+            floored[i] = small.tile([P, 1], F32, tag="floored", name="floored")
+            nc.vector.tensor_scalar_max(floored[i][:], norm[i][:], EPS)
+
         def invert_norm(i):
-            floored = small.tile([P, 1], F32, tag="floored")
-            nc.vector.tensor_scalar_max(floored[:], norm[i][:], EPS)
             inverse[i] = small.tile([P, 1], F32, tag="inverse", name="inverse")
-            nc.vector.reciprocal(inverse[i][:], floored[:])
+            nc.vector.reciprocal(inverse[i][:], floored[i][:])
 
         def round_message(i):
-            for g, first, last in ((0, 0, P * PACK), (1, P * PACK, MESSAGE)):
-                planes = mu_planes[:, i, g, :, 0 : (last - first) // PACK].rearrange("b t p -> b p t")
-                columns = z[i][:, first:last].rearrange("b (p t) -> b p t", t=PACK)
-                if i < LAG:
-                    nc.gpsimd.tensor_scalar(
-                        out=planes,
-                        in0=columns,
-                        scalar1=inverse[i][:],
-                        scalar2=0.0,
-                        op0=ALU.mult,
-                        op1=ALU.add,
-                    )
-                else:
-                    nc.scalar.activation(out=planes, in_=columns, func=ACT.Copy, scale=inverse[i][:])
+            nc.vector.tensor_scalar(
+                out=mu[:, i, 0:MESSAGE], in0=z[i][:], scalar1=inverse[i][:], scalar2=None, op0=ALU.mult
+            )
 
         def flip_mu(i):
-            mu_flipped[i] = psum.tile([P, PASSES, PACK, P], BF16, tag="bank", name="mu_flipped")
-            for g in range(PASSES):
-                for t in range(PACK):
-                    nc.tensor.transpose(
-                        mu_flipped[i][:, g, t, :], mu_planes[:, i, g, t, :], identity_bf16[:]
-                    )
+            mu_flipped[i] = flip(mu[:, i, :].bitcast(F32))
 
-        def group_mu(i):
-            mu_grouped[i] = work.tile(
-                [P, PASSES, P, PACK], BF16, tag="mu_grouped", name="mu_grouped", align_bytes=64
-            )
-            nc.scalar.copy(out=mu_grouped[i][:], in_=mu_flipped[i][:].rearrange("p g t b -> p g b t"))
+        def empty_mu(i):
+            mu_grouped[i] = new_group(1)
+            empty(on_scalar, mu_flipped[i], mu_grouped[i], 0)
 
         def quantise_mu(i):
-            nc.vector.quantize_mx(
-                out=mu_codes[:, i].rearrange("p g b -> p (g b)").bitcast(FP8X4),
-                scales=mu_scales[:, i].rearrange("p g b -> p (g b)"),
-                in_=mu_grouped[i][:].rearrange("p g b t -> p (g b t)"),
-            )
+            quantise_stationary(mu_grouped[i], mu_codes[:, i], mu_scales[:, i])
 
-        def link(stage, i):
-            if 0 <= i < B_TILES:
-                stage(i)
+        result, acc = {}, {}
 
-        result = {}
-
-        def second_matmul(i, n):
-            w1 = w1_groups[n]
-            acc = psum.tile([P, BANK], F32, tag="bank")
-            for g in range(PASSES):
-                nc.tensor.matmul_mx(
-                    out=acc[:],
-                    lhsT=mu_codes[:, i, g, :].bitcast(FP8X4),
-                    lhsT_scale=mu_scales[:, i, g, :],
-                    rhs=w1["codes"][:, g, :].bitcast(FP8X4),
-                    rhs_scale=w1["scales"][:, g, :],
-                    start=(g == 0),
-                    stop=(g == PASSES - 1),
-                )
-            side = n % 2
-            if side == 0:
-                result[i] = results.tile([P, 2 * BANK], F32, tag="result", name="result")
-            nc.vector.tensor_tensor(
-                out=result[i][:, side * BANK : (side + 1) * BANK],
-                in0=acc[:],
-                in1=bias_all[:, B1_START + n * BANK : B1_START + (n + 1) * BANK],
-                op=ALU.add,
-            )
-            if side == 1:
-                if i < LAG:
-                    nc.gpsimd.tensor_scalar(
-                        out=result[i][:],
-                        in0=result[i][:],
-                        scalar1=math.inf,
-                        scalar2=0.0,
-                        op0=ALU.min,
-                        op1=ALU.max,
+        def multiply_unit(i, h):
+            for n in (2 * h, 2 * h + 1):
+                acc[i, n] = psum.tile([P, BANK], F32, tag="bank", name="acc")
+                for g in range(PASSES):
+                    nc.tensor.matmul_mx(
+                        out=acc[i, n][:],
+                        lhsT=mu_codes[:, i, g, :].bitcast(FP8X4),
+                        lhsT_scale=mu_scales[:, i, g, :],
+                        rhs=w1_codes[n][:, g, :].bitcast(FP8X4),
+                        rhs_scale=w1_scales[n][:, g, :],
+                        start=(g == 0),
+                        stop=(g == PASSES - 1),
                     )
-                else:
-                    nc.scalar.activation(out=result[i][:], in_=result[i][:], func=ACT.Relu)
-                nc.sync.dma_start(
-                    out=out_tiles[i // GROUP, i % GROUP, :, (n - 1) * BANK : (n + 1) * BANK],
-                    in_=result[i][:],
+
+        def add_unit(i, h):
+            result[i, h] = results.tile([P, 2 * BANK], F32, tag="result", name="result")
+            for n in (2 * h, 2 * h + 1):
+                nc.vector.tensor_tensor(
+                    out=result[i, h][:, (n % 2) * BANK : (n % 2 + 1) * BANK],
+                    in0=acc[i, n][:],
+                    in1=bias2[:, n * BANK : (n + 1) * BANK],
+                    op=ALU.add,
                 )
 
-        def bulk_quarter(step, quarter):
-            if step <= W1_GROUPS and quarter == 1:
-                quantise_group(nc, groups[-1])
-            if step < W1_GROUPS:
-                if quarter == 0:
-                    w1_groups.append(new_group(pools, w1_rows[step], WORDS_IN_TURN, "w1_%d" % step))
-                flip_row_tile(nc, pools, identity_f32, w1_groups[step], quarter)
-                if quarter == GROUP - 1:
-                    groups.append(w1_groups[step])
-            if step >= LAG:
-                second_matmul(step - LAG, quarter)
+        def store_unit(i, h, on_gpsimd):
+            if on_gpsimd:
+                for half in range(2):
+                    part = result[i, h][:, half * BANK : (half + 1) * BANK]
+                    nc.gpsimd.tensor_scalar(
+                        out=part, in0=part, scalar1=math.inf, scalar2=0.0, op0=ALU.min, op1=ALU.max
+                    )
+            else:
+                nc.scalar.activation(out=result[i, h][:], in_=result[i, h][:], func=ACT.Relu)
+            nc.sync.dma_start(
+                out=out_tiles[i // 2, i % 2, :, h * 2 * BANK : (h + 1) * 2 * BANK], in_=result[i, h][:]
+            )
 
-        nc.vector.tensor_copy(
-            out=mu_planes[:, :, 1, :, message_p:P],
-            in_=action_sb[:].rearrange("b i (p t) -> b i t p", t=PACK),
-        )
+        w3_grouped = [new_group(n) for n in W3_GROUP_TILES]
 
-        for step in range(B_TILES + LAG):
-            link(invert_norm, step - 1)
-            link(flip_mu, step - 2)
-            link(first_matmul, step)
-            bulk_quarter(step, 0)
-            link(round_message, step - 1)
-            link(add_first_bias, step)
-            bulk_quarter(step, 1)
-            link(group_mu, step - 2)
-            link(quantise_mu, step - 3)
-            bulk_quarter(step, 2)
-            link(take_norm, step)
-            bulk_quarter(step, 3)
+        def quantise_w3(group):
+            for g in range(PASSES):
+                quantise(w3_grouped[group][:, g], w3_codes[group][:, g, :], w3_scales[group][:, g, :])
+
+        group_of_tile = [group for group, n in enumerate(W3_GROUP_TILES) for j in range(n)]
+        for j in range(W3_TILES):
+            group = group_of_tile[j]
+            empty(
+                on_vector if j % 2 else on_scalar, flip(w3_rows[j][:].bitcast(F32)), w3_grouped[group],
+                j - W3_GROUP_START[group],
+            )
+            if j == 4:
+                quantise_w3(0)
+            if j == 6:
+                quantise_w3(1)
+        flip_x(0)
+        empty_x(0)
+        quantise_w3(2)
+        quantise_x(0)
+
+        units = [(0, 0), (1, 0), (0, 1), (2, 0), (1, 1), (2, 1)] + [(i, h) for i in range(3, B_TILES) for h in range(2)]
+        quota = [(0, 0), (0, 0), (0, 0), (1, 1), (0, 2), (1, 1), (1, 1), (1, 1), (1, 1), (1, 1), (1, 1)]
+        taken, added, stored = [], [], []
+
+        def multiply_units(count):
+            for unit in units[len(taken) : len(taken) + count]:
+                multiply_unit(unit[0], unit[1])
+                taken.append(unit)
+
+        def store_units():
+            while len(stored) < len(added):
+                i, h = added[len(stored)]
+                store_unit(i, h, step>=4 and len(stored)%2==0)
+                stored.append((i, h))
+
+        def add_units():
+            for unit in taken[len(added):]:
+                add_unit(unit[0], unit[1])
+                added.append(unit)
+
+        for step in range(B_TILES + LAG + 1):
+            w1 = GROUP * step if step < W1_GROUPS else None
+            chain = step - LAG
+            if chain >= B_TILES: chain=-1
+            before = 0 <= step - 1 < B_TILES
+            flip_x(step + 1)
+            empty_x(step + 1)
+            if chain >= 0:
+                flip_mu(chain)
+                empty_mu(chain)
+            if before: take_norm(step-1)
+            store_units()
+            quantise_x(step + 1)
+            if w1 is not None:
+                flip_w1(w1)
+                empty_w1(w1, on_scalar)
+                flip_w1(w1 + 1)
+                empty_w1(w1 + 1, on_scalar)
+            if chain >= 0:
+                quantise_mu(chain)
+            if 1 <= step <= W1_GROUPS:
+                quantise_w1(2 * step - 2)
+                quantise_w1(2 * step - 1)
+            multiply_units(quota[step][0])
+            add_units()
+            if before: floor_norm(step-1)
+            if step < B_TILES:
+                first_matmul(step)
+            if w1 is not None:
+                flip_w1(w1 + 2)
+                flip_w1(w1 + 3)
+                empty_w1(w1 + 2, on_scalar)
+            store_units()
+            if step < B_TILES:
+                add_first_bias(step, lambda: invert_norm(step-1) if before else None)
+            elif before: invert_norm(step-1)
+            if w1 is not None:
+                empty_w1(w1 + 3, on_scalar)
+            if before: round_message(step-1)
+            multiply_units(quota[step][1])
+            add_units()
+        store_units()

@@ -22,7 +22,6 @@ BANK = 512
 
 BATCH = 1024
 MESSAGE = 896
-ACTION = K - MESSAGE
 OUT = 2048
 EPS = 1e-12
 
@@ -32,8 +31,6 @@ W1_GROUPS = OUT // BANK
 W3_TILES = MESSAGE // P
 W3_GROUP_TILES = (4, 2, 1)
 W3_GROUP_START = (0, 4, 6)
-
-LAG = 2
 
 FLOPS = 2 * BATCH * K * (MESSAGE + OUT)
 
@@ -45,19 +42,12 @@ def tile_modelgraphpolicy_pb_kernel(tc, xum, action, up_w3, up_b3, dyn_w1_mu, dy
         raw = ctx.enter_context(tc.tile_pool(name="raw", bufs=1))
         operands = ctx.enter_context(tc.tile_pool(name="operands", bufs=1))
         grouped_pool = ctx.enter_context(tc.tile_pool(name="grouped", bufs=4))
-        work = ctx.enter_context(tc.tile_pool(name="work", bufs=3))
-        small = ctx.enter_context(tc.tile_pool(name="small", bufs=3))
+        wide_pool = ctx.enter_context(tc.tile_pool(name="wide", bufs=1))
+        work = ctx.enter_context(tc.tile_pool(name="work", bufs=4))
+        small = ctx.enter_context(tc.tile_pool(name="small", bufs=4))
         results = ctx.enter_context(tc.tile_pool(name="results", bufs=6))
         psum = ctx.enter_context(tc.psum_pool(name="psum", bufs=8))
         ctx.enter_context(tc.manual_schedule())
-
-        bias1 = const.tile([P, MESSAGE], BF16)
-        bias2 = const.tile([P, OUT], BF16)
-
-        def load_pair(rows, row_order, name):
-            pair = raw.tile([P, 2, K], BF16, name=name)
-            nc.sync.dma_start(out=pair[:], in_=rows.rearrange(row_order, r=P))
-            return pair
 
         w3_rows = []
         for j in range(W3_TILES):
@@ -68,48 +58,52 @@ def tile_modelgraphpolicy_pb_kernel(tc, xum, action, up_w3, up_b3, dyn_w1_mu, dy
         x_pairs = {}
         w1_pairs = {}
         mu = raw.tile([P, B_TILES, K], BF16)
+        bias1 = const.tile([P, MESSAGE], BF16)
+        bias2 = const.tile([P, OUT], BF16)
 
         def load_x(s):
-            x_pairs[s] = load_pair(xum[2 * P * s : 2 * P * (s + 1), :], "(r j) k -> r j k", "x_rows%d" % s)
+            x_pairs[s] = raw.tile([P, 2, K], BF16, name="x_rows%d" % s)
+            nc.sync.dma_start(
+                out=x_pairs[s][:], in_=xum[2 * P * s : 2 * P * (s + 1), :].rearrange("(r j) k -> r j k", j=2)
+            )
 
-        def load_w1(n):
-            for s in (2 * n, 2 * n + 1):
-                w1_pairs[s] = load_pair(
-                    dyn_w1_mu[2 * P * s : 2 * P * (s + 1), :], "(j r) k -> r j k", "w1_rows%d" % s
-                )
+        def load_w1(s):
+            w1_pairs[s] = raw.tile([P, 2, K], BF16, name="w1_rows%d" % s)
+            nc.sync.dma_start(
+                out=w1_pairs[s][:], in_=dyn_w1_mu[2 * P * s : 2 * P * (s + 1), :].rearrange("(j r) k -> r j k", j=2)
+            )
 
-        load_x(0)
-        nc.sync.dma_start(out=bias1[:], in_=up_b3.partition_broadcast(P))
-        load_w1(0)
-        load_x(1)
-        load_w1(1)
+        for s in range(B_TILES // 2):
+            load_x(s)
+            if s == 0:
+                nc.sync.dma_start(out=bias1[:], in_=up_b3.partition_broadcast(P))
+            load_w1(s)
         for s in range(B_TILES // 2):
             nc.sync.dma_start(
                 out=mu[:, 2 * s : 2 * s + 2, MESSAGE:K],
                 in_=action[2 * P * s : 2 * P * (s + 1), :].rearrange("(r j) a -> r j a", j=2),
             )
-        load_w1(2)
-        load_x(2)
-        load_w1(3)
         nc.sync.dma_start(out=bias2[:], in_=dyn_b1.partition_broadcast(P))
-        load_x(3)
+        for s in range(B_TILES // 2, B_TILES):
+            load_w1(s)
         out_tiles = out.rearrange("(s r j) n -> s j r n", r=P, j=2)
 
-        identity_f32 = const.tile([P, P], F32)
-        make_identity(nc, identity_f32[:])
+        identity = const.tile([P, P], F32)
+        make_identity(nc, identity[:])
         one = const.tile([P, 1], F32)
         nc.vector.memset(one[:], 1.0)
         nc.scalar.sqrt(one[:], one[:])
+
+        on_scalar = nc.scalar.copy
+        on_vector = nc.vector.tensor_copy
 
         def flip(words):
             flipped = psum.tile([P, PASSES, PAIRS, P], F32, tag="bank", name="flipped")
             turned = words.rearrange("r (g p u) -> r g u p", g=PASSES, u=PAIRS)
             for g in range(PASSES):
                 for u in range(PAIRS):
-                    nc.tensor.transpose(flipped[:, g, u, :], turned[:, g, u, :], identity_f32[:])
+                    nc.tensor.transpose(flipped[:, g, u, :], turned[:, g, u, :], identity[:])
             return flipped
-
-        wide_pool = ctx.enter_context(tc.tile_pool(name="wide", bufs=1))
 
         def new_group(tiles):
             pool = grouped_pool if tiles < GROUP else wide_pool
@@ -118,15 +112,11 @@ def tile_modelgraphpolicy_pb_kernel(tc, xum, action, up_w3, up_b3, dyn_w1_mu, dy
             )
 
         def empty(copy, flipped, grouped, j):
+            rows = grouped[:, :, j * P : (j + 1) * P, :].rearrange("p g r t -> p g (r t)")
             copy(
-                out=grouped[:, :, j * P : (j + 1) * P, :].rearrange("p g r t -> p g (r t)").bitcast(F32).rearrange(
-                    "p g (r u) -> p g r u", u=PAIRS
-                ),
+                out=rows.bitcast(F32).rearrange("p g (r u) -> p g r u", u=PAIRS),
                 in_=flipped[:].rearrange("p g u r -> p g r u"),
             )
-
-        on_scalar = nc.scalar.copy
-        on_vector = nc.vector.tensor_copy
 
         def quantise(grouped, codes, scales):
             nc.vector.quantize_mx(
@@ -161,17 +151,14 @@ def tile_modelgraphpolicy_pb_kernel(tc, xum, action, up_w3, up_b3, dyn_w1_mu, dy
         z_ps, z, norm, floored, inverse, mu_flipped, mu_grouped = {}, {}, {}, {}, {}, {}, {}
 
         def flip_x(i):
-            if i < B_TILES:
-                x_flipped[i] = flip(x_pairs[i // 2][:, i % 2, :].bitcast(F32))
+            x_flipped[i] = flip(x_pairs[i // 2][:, i % 2, :].bitcast(F32))
 
         def empty_x(i):
-            if i < B_TILES:
-                x_grouped[i] = new_group(1)
-                empty(on_scalar, x_flipped[i], x_grouped[i], 0)
+            x_grouped[i] = new_group(1)
+            empty(on_scalar, x_flipped[i], x_grouped[i], 0)
 
         def quantise_x(i):
-            if i < B_TILES:
-                quantise_stationary(x_grouped[i], x_codes[:, i], x_scales[:, i])
+            quantise_stationary(x_grouped[i], x_codes[:, i], x_scales[:, i])
 
         def flip_w1(j):
             w1_flipped[j] = flip(w1_pairs[j // 2][:, j % 2, :].bitcast(F32))
@@ -203,16 +190,13 @@ def tile_modelgraphpolicy_pb_kernel(tc, xum, action, up_w3, up_b3, dyn_w1_mu, dy
                         stop=(g == PASSES - 1),
                     )
 
-        def add_first_bias(i, between=lambda: None):
-            z[i] = work.tile([P, MESSAGE], F32, tag="z", name="z")
-            for h, first, last in ((0, 0, BANK), (1, BANK, MESSAGE)):
-                if h == 1: between()
-                nc.vector.tensor_tensor(
-                    out=z[i][:, first:last],
-                    in0=z_ps[i][h][:, 0 : last - first],
-                    in1=bias1[:, first:last],
-                    op=ALU.add,
-                )
+        def add_first_bias(i, h):
+            first, last = h * BANK, min((h + 1) * BANK, MESSAGE)
+            if h == 0:
+                z[i] = work.tile([P, MESSAGE], F32, tag="z", name="z")
+            nc.vector.tensor_tensor(
+                out=z[i][:, first:last], in0=z_ps[i][h][:, 0 : last - first], in1=bias1[:, first:last], op=ALU.add
+            )
 
         def take_norm(i):
             squares = work.tile([P, MESSAGE], F32, tag="squares", name="squares")
@@ -230,9 +214,10 @@ def tile_modelgraphpolicy_pb_kernel(tc, xum, action, up_w3, up_b3, dyn_w1_mu, dy
             nc.vector.reciprocal(inverse[i][:], floored[i][:])
 
         def round_message(i):
-            nc.vector.tensor_scalar(
-                out=mu[:, i, 0:MESSAGE], in0=z[i][:], scalar1=inverse[i][:], scalar2=None, op0=ALU.mult
-            )
+            if False:
+                nc.scalar.activation(out=mu[:, i, 0:MESSAGE], in_=z[i][:], func=ACT.Copy, scale=inverse[i][:])
+            else:
+                nc.vector.tensor_scalar_mul(mu[:, i, 0:MESSAGE], z[i][:], inverse[i][:])
 
         def flip_mu(i):
             mu_flipped[i] = flip(mu[:, i, :].bitcast(F32))
@@ -246,42 +231,46 @@ def tile_modelgraphpolicy_pb_kernel(tc, xum, action, up_w3, up_b3, dyn_w1_mu, dy
 
         result, acc = {}, {}
 
-        def multiply_unit(i, h):
-            for n in (2 * h, 2 * h + 1):
-                acc[i, n] = psum.tile([P, BANK], F32, tag="bank", name="acc")
-                for g in range(PASSES):
-                    nc.tensor.matmul_mx(
-                        out=acc[i, n][:],
-                        lhsT=mu_codes[:, i, g, :].bitcast(FP8X4),
-                        lhsT_scale=mu_scales[:, i, g, :],
-                        rhs=w1_codes[n][:, g, :].bitcast(FP8X4),
-                        rhs_scale=w1_scales[n][:, g, :],
-                        start=(g == 0),
-                        stop=(g == PASSES - 1),
-                    )
-
-        def add_unit(i, h):
-            result[i, h] = results.tile([P, 2 * BANK], F32, tag="result", name="result")
-            for n in (2 * h, 2 * h + 1):
-                nc.vector.tensor_tensor(
-                    out=result[i, h][:, (n % 2) * BANK : (n % 2 + 1) * BANK],
-                    in0=acc[i, n][:],
-                    in1=bias2[:, n * BANK : (n + 1) * BANK],
-                    op=ALU.add,
+        def multiply(i, n):
+            acc[i, n] = psum.tile([P, BANK], F32, tag="bank", name="acc")
+            for g in range(PASSES):
+                nc.tensor.matmul_mx(
+                    out=acc[i, n][:],
+                    lhsT=mu_codes[:, i, g, :].bitcast(FP8X4),
+                    lhsT_scale=mu_scales[:, i, g, :],
+                    rhs=w1_codes[n][:, g, :].bitcast(FP8X4),
+                    rhs_scale=w1_scales[n][:, g, :],
+                    start=(g == 0),
+                    stop=(g == PASSES - 1),
                 )
 
-        def store_unit(i, h, on_gpsimd):
-            if on_gpsimd:
-                for half in range(2):
-                    part = result[i, h][:, half * BANK : (half + 1) * BANK]
-                    nc.gpsimd.tensor_scalar(
-                        out=part, in0=part, scalar1=math.inf, scalar2=0.0, op0=ALU.min, op1=ALU.max
-                    )
-            else:
-                nc.scalar.activation(out=result[i, h][:], in_=result[i, h][:], func=ACT.Relu)
-            nc.sync.dma_start(
-                out=out_tiles[i // 2, i % 2, :, h * 2 * BANK : (h + 1) * 2 * BANK], in_=result[i, h][:]
+        def add_second_bias(i, n):
+            if n % 2 == 0:
+                result[i, n // 2] = results.tile([P, 2 * BANK], F32, tag="result", name="result")
+            nc.vector.tensor_tensor(
+                out=result[i, n // 2][:, (n % 2) * BANK : (n % 2 + 1) * BANK],
+                in0=acc[i, n][:],
+                in1=bias2[:, n * BANK : (n + 1) * BANK],
+                op=ALU.add,
             )
+
+        def relu(part, on_gpsimd):
+            if on_gpsimd:
+                nc.gpsimd.tensor_scalar(
+                    out=part, in0=part, scalar1=math.inf, scalar2=0.0, op0=ALU.min, op1=ALU.max
+                )
+            else:
+                nc.scalar.activation(out=part, in_=part, func=ACT.Relu)
+
+        def store(i, first, last):
+            start = first // 2 * 2 * BANK
+            nc.sync.dma_start(
+                out=out_tiles[i // 2, i % 2, :, first * BANK : last * BANK],
+                in_=result[i, first // 2][:, first * BANK - start : last * BANK - start],
+            )
+
+        def half_of(i, n):
+            return result[i, n // 2][:, (n % 2) * BANK : (n % 2 + 1) * BANK]
 
         w3_grouped = [new_group(n) for n in W3_GROUP_TILES]
 
@@ -293,7 +282,9 @@ def tile_modelgraphpolicy_pb_kernel(tc, xum, action, up_w3, up_b3, dyn_w1_mu, dy
         for j in range(W3_TILES):
             group = group_of_tile[j]
             empty(
-                on_vector if j % 2 else on_scalar, flip(w3_rows[j][:].bitcast(F32)), w3_grouped[group],
+                on_vector if j % 2 == 1 else on_scalar,
+                flip(w3_rows[j][:].bitcast(F32)),
+                w3_grouped[group],
                 j - W3_GROUP_START[group],
             )
             if j == 4:
@@ -305,65 +296,87 @@ def tile_modelgraphpolicy_pb_kernel(tc, xum, action, up_w3, up_b3, dyn_w1_mu, dy
         quantise_w3(2)
         quantise_x(0)
 
-        units = [(0, 0), (1, 0), (0, 1), (2, 0), (1, 1), (2, 1)] + [(i, h) for i in range(3, B_TILES) for h in range(2)]
-        quota = [(0, 0), (0, 0), (0, 0), (1, 1), (0, 2), (1, 1), (1, 1), (1, 1), (1, 1), (1, 1), (1, 1)]
-        taken, added, stored = [], [], []
+        def chain(i):
+            floor_norm(i)
+            invert_norm(i)
+            round_message(i)
 
-        def multiply_units(count):
-            for unit in units[len(taken) : len(taken) + count]:
-                multiply_unit(unit[0], unit[1])
-                taken.append(unit)
+        for i in range(B_TILES):
+            if i + 1 < B_TILES:
+                flip_x(i + 1)
+                empty_x(i + 1)
+            else:
+                flip_mu(0)
+                empty_mu(0)
+            flip_w1(i)
+            if i >= 2:
+                floor_norm(i - 2)
+            if i >= 1:
+                add_first_bias(i - 1, 0)
+                if i >= 2:
+                    invert_norm(i - 2)
+                add_first_bias(i - 1, 1)
+                take_norm(i - 1)
+            empty_w1(i, on_scalar)
+            if i + 1 < B_TILES:
+                quantise_x(i + 1)
+            else:
+                quantise_mu(0)
+            first_matmul(i)
+            if i >= 2:
+                round_message(i - 2)
+            if i % 2 == 0 and i > 0:
+                quantise_w1(i // 2 - 1)
 
-        def store_units():
-            while len(stored) < len(added):
-                i, h = added[len(stored)]
-                store_unit(i, h, step>=4 and len(stored)%2==0)
-                stored.append((i, h))
+        w1_tiles = [(8, 9), (10,), (11,), (12,), (13,), (14,), (15,), ()]
+        ready = []
+        for c in range(B_TILES):
+            if c + 1 < B_TILES:
+                flip_mu(c + 1)
+                empty_mu(c + 1)
+            for j in w1_tiles[c]:
+                flip_w1(j)
+            if c == 0:
+                quantise_w1(3)
+                floor_norm(B_TILES - 2)
+                add_first_bias(B_TILES - 1, 0)
+                invert_norm(B_TILES - 2)
+                add_first_bias(B_TILES - 1, 1)
+                take_norm(B_TILES - 1)
+                round_message(B_TILES - 2)
+            if c == 1:
+                floor_norm(B_TILES - 1)
+            if c == 1:
+                invert_norm(B_TILES - 1)
+            if c > 0:
+                relu(half_of(c - 1, 0), False)
+                relu(half_of(c - 1, 1), False)
+                store(c - 1, 0, 2)
+            for j in w1_tiles[c]:
+                empty_w1(j, on_scalar)
+                if j % 2 == 1:
+                    ready.append(j // 2)
+            if c == 1:
+                round_message(B_TILES - 1)
+            for n in (0, 1):
+                multiply(c, n)
+                add_second_bias(c, n)
+            if c + 1 < B_TILES:
+                quantise_mu(c + 1)
+            for s in ready:
+                quantise_w1(s)
+            ready = []
 
-        def add_units():
-            for unit in taken[len(added):]:
-                add_unit(unit[0], unit[1])
-                added.append(unit)
-
-        for step in range(B_TILES + LAG + 1):
-            w1 = GROUP * step if step < W1_GROUPS else None
-            chain = step - LAG
-            if chain >= B_TILES: chain=-1
-            before = 0 <= step - 1 < B_TILES
-            flip_x(step + 1)
-            empty_x(step + 1)
-            if chain >= 0:
-                flip_mu(chain)
-                empty_mu(chain)
-            if before: take_norm(step-1)
-            store_units()
-            quantise_x(step + 1)
-            if w1 is not None:
-                flip_w1(w1)
-                empty_w1(w1, on_scalar)
-                flip_w1(w1 + 1)
-                empty_w1(w1 + 1, on_scalar)
-            if chain >= 0:
-                quantise_mu(chain)
-            if 1 <= step <= W1_GROUPS:
-                quantise_w1(2 * step - 2)
-                quantise_w1(2 * step - 1)
-            multiply_units(quota[step][0])
-            add_units()
-            if before: floor_norm(step-1)
-            if step < B_TILES:
-                first_matmul(step)
-            if w1 is not None:
-                flip_w1(w1 + 2)
-                flip_w1(w1 + 3)
-                empty_w1(w1 + 2, on_scalar)
-            store_units()
-            if step < B_TILES:
-                add_first_bias(step, lambda: invert_norm(step-1) if before else None)
-            elif before: invert_norm(step-1)
-            if w1 is not None:
-                empty_w1(w1 + 3, on_scalar)
-            if before: round_message(step-1)
-            multiply_units(quota[step][1])
-            add_units()
-        store_units()
+        relu(half_of(B_TILES - 1, 0), False)
+        relu(half_of(B_TILES - 1, 1), True)
+        store(B_TILES - 1, 0, 2)
+        for c in range(B_TILES):
+            for n in (2, 3):
+                multiply(c, n)
+                add_second_bias(c, n)
+                if c == B_TILES - 1:
+                    relu(half_of(c, n), n==2)
+                    store(c, n, n + 1)
+                elif n == 3:
+                    relu(result[c, 1][:], c % 2 == 0)
+                    store(c, 2, 4)

@@ -28,6 +28,7 @@ EPS = 1e-12
 B_TILES = BATCH // P
 GROUP = BANK // P
 W1_GROUPS = OUT // BANK
+W1_PAIRS = OUT // (2 * P)
 W3_TILES = MESSAGE // P
 W3_GROUP_TILES = (4, 2, 1)
 W3_GROUP_START = (0, 4, 6)
@@ -43,9 +44,9 @@ def tile_modelgraphpolicy_pb_kernel(tc, xum, action, up_w3, up_b3, dyn_w1_mu, dy
         operands = ctx.enter_context(tc.tile_pool(name="operands", bufs=1))
         grouped_pool = ctx.enter_context(tc.tile_pool(name="grouped", bufs=4))
         wide_pool = ctx.enter_context(tc.tile_pool(name="wide", bufs=1))
-        work = ctx.enter_context(tc.tile_pool(name="work", bufs=4))
+        work = ctx.enter_context(tc.tile_pool(name="work", bufs=5))
         small = ctx.enter_context(tc.tile_pool(name="small", bufs=4))
-        results = ctx.enter_context(tc.tile_pool(name="results", bufs=6))
+        results = ctx.enter_context(tc.tile_pool(name="results", bufs=9))
         psum = ctx.enter_context(tc.psum_pool(name="psum", bufs=8))
         ctx.enter_context(tc.manual_schedule())
 
@@ -73,19 +74,21 @@ def tile_modelgraphpolicy_pb_kernel(tc, xum, action, up_w3, up_b3, dyn_w1_mu, dy
                 out=w1_pairs[s][:], in_=dyn_w1_mu[2 * P * s : 2 * P * (s + 1), :].rearrange("(j r) k -> r j k", j=2)
             )
 
-        for s in range(B_TILES // 2):
-            load_x(s)
+        load_x(0)
+        load_x(1)
+        for s in range(W1_PAIRS):
+            load_w1(s)
             if s == 0:
                 nc.sync.dma_start(out=bias1[:], in_=up_b3.partition_broadcast(P))
-            load_w1(s)
-        for s in range(B_TILES // 2):
-            nc.sync.dma_start(
-                out=mu[:, 2 * s : 2 * s + 2, MESSAGE:K],
-                in_=action[2 * P * s : 2 * P * (s + 1), :].rearrange("(r j) a -> r j a", j=2),
-            )
-        nc.sync.dma_start(out=bias2[:], in_=dyn_b1.partition_broadcast(P))
-        for s in range(B_TILES // 2, B_TILES):
-            load_w1(s)
+            if s == 1 or s == 3:
+                load_x(s // 2 + 2)
+            if s == 4:
+                for t in range(B_TILES // 2):
+                    nc.sync.dma_start(
+                        out=mu[:, 2 * t : 2 * t + 2, MESSAGE:K],
+                        in_=action[2 * P * t : 2 * P * (t + 1), :].rearrange("(r j) a -> r j a", j=2),
+                    )
+                nc.sync.dma_start(out=bias2[:], in_=dyn_b1.partition_broadcast(P))
         out_tiles = out.rearrange("(s r j) n -> s j r n", r=P, j=2)
 
         identity = const.tile([P, P], F32)
@@ -199,7 +202,7 @@ def tile_modelgraphpolicy_pb_kernel(tc, xum, action, up_w3, up_b3, dyn_w1_mu, dy
             )
 
         def take_norm(i):
-            squares = work.tile([P, MESSAGE], F32, tag="squares", name="squares")
+            squares = wide_pool.tile([P, MESSAGE], F32, tag="squares", name="squares")
             sum_squares = small.tile([P, 1], F32, tag="sum_squares", name="sum_squares")
             nc.scalar.activation(out=squares[:], in_=z[i][:], func=ACT.Square, accum_out=sum_squares[:])
             norm[i] = small.tile([P, 1], F32, tag="norm", name="norm")
@@ -214,8 +217,15 @@ def tile_modelgraphpolicy_pb_kernel(tc, xum, action, up_w3, up_b3, dyn_w1_mu, dy
             nc.vector.reciprocal(inverse[i][:], floored[i][:])
 
         def round_message(i):
-            if False:
-                nc.scalar.activation(out=mu[:, i, 0:MESSAGE], in_=z[i][:], func=ACT.Copy, scale=inverse[i][:])
+            if i < 6:
+                nc.gpsimd.tensor_scalar(
+                    out=mu[:, i, 0:MESSAGE],
+                    in0=z[i][:],
+                    scalar1=inverse[i][:],
+                    scalar2=0.0,
+                    op0=ALU.mult,
+                    op1=ALU.add,
+                )
             else:
                 nc.vector.tensor_scalar_mul(mu[:, i, 0:MESSAGE], z[i][:], inverse[i][:])
 
@@ -294,89 +304,79 @@ def tile_modelgraphpolicy_pb_kernel(tc, xum, action, up_w3, up_b3, dyn_w1_mu, dy
         flip_x(0)
         empty_x(0)
         quantise_w3(2)
+        flip_x(1)
+        empty_x(1)
         quantise_x(0)
+        quantise_x(1)
 
-        def chain(i):
-            floor_norm(i)
-            invert_norm(i)
-            round_message(i)
+        w1_flipped_count, w1_emptied_count, w1_done_count = [], [], []
 
-        for i in range(B_TILES):
-            if i + 1 < B_TILES:
-                flip_x(i + 1)
-                empty_x(i + 1)
-            else:
-                flip_mu(0)
-                empty_mu(0)
-            flip_w1(i)
-            if i >= 2:
-                floor_norm(i - 2)
-            if i >= 1:
-                add_first_bias(i - 1, 0)
-                if i >= 2:
-                    invert_norm(i - 2)
-                add_first_bias(i - 1, 1)
-                take_norm(i - 1)
-            empty_w1(i, on_scalar)
-            if i + 1 < B_TILES:
-                quantise_x(i + 1)
-            else:
-                quantise_mu(0)
-            first_matmul(i)
-            if i >= 2:
-                round_message(i - 2)
-            if i % 2 == 0 and i > 0:
-                quantise_w1(i // 2 - 1)
+        def flip_next_w1(count):
+            for n in range(count):
+                flip_w1(len(w1_flipped_count))
+                w1_flipped_count.append(None)
 
-        w1_tiles = [(8, 9), (10,), (11,), (12,), (13,), (14,), (15,), ()]
-        ready = []
-        for c in range(B_TILES):
-            if c + 1 < B_TILES:
-                flip_mu(c + 1)
-                empty_mu(c + 1)
-            for j in w1_tiles[c]:
-                flip_w1(j)
-            if c == 0:
-                quantise_w1(3)
-                floor_norm(B_TILES - 2)
-                add_first_bias(B_TILES - 1, 0)
-                invert_norm(B_TILES - 2)
-                add_first_bias(B_TILES - 1, 1)
-                take_norm(B_TILES - 1)
-                round_message(B_TILES - 2)
-            if c == 1:
-                floor_norm(B_TILES - 1)
-            if c == 1:
-                invert_norm(B_TILES - 1)
-            if c > 0:
-                relu(half_of(c - 1, 0), False)
-                relu(half_of(c - 1, 1), False)
-                store(c - 1, 0, 2)
-            for j in w1_tiles[c]:
-                empty_w1(j, on_scalar)
-                if j % 2 == 1:
-                    ready.append(j // 2)
-            if c == 1:
-                round_message(B_TILES - 1)
-            for n in (0, 1):
-                multiply(c, n)
-                add_second_bias(c, n)
-            if c + 1 < B_TILES:
-                quantise_mu(c + 1)
-            for s in ready:
-                quantise_w1(s)
-            ready = []
+        def empty_next_w1():
+            while len(w1_emptied_count) < len(w1_flipped_count):
+                j = len(w1_emptied_count)
+                empty_w1(j, on_vector if False else on_scalar)
+                w1_emptied_count.append(None)
 
-        relu(half_of(B_TILES - 1, 0), False)
-        relu(half_of(B_TILES - 1, 1), True)
-        store(B_TILES - 1, 0, 2)
-        for c in range(B_TILES):
-            for n in (2, 3):
-                multiply(c, n)
-                add_second_bias(c, n)
-                if c == B_TILES - 1:
-                    relu(half_of(c, n), n==2)
-                    store(c, n, n + 1)
-                elif n == 3:
-                    relu(result[c, 1][:], c % 2 == 0)
-                    store(c, 2, 4)
+        def quantise_next_w1(pairs):
+            while len(w1_done_count) < pairs:
+                quantise_w1(len(w1_done_count))
+                w1_done_count.append(None)
+
+        w1_tiles = [2,2,2,2,1,1,2,2,2]
+        unit_counts = [0,0,0,0,0,1,1,1,1,1,2,2,2,2,2,1]
+        units = [(i, 0) for i in range(6)] + [(0, 1), (6, 0), (1, 1), (7, 0)] + [(i, 1) for i in range(2, B_TILES)]
+        multiplied, stored = [], []
+
+        def store_units(keep):
+            while len(stored) < len(multiplied) - keep:
+                i, h = multiplied[len(stored)]
+                for n in (2 * h, 2 * h + 1):
+                    relu(half_of(i, n), n % 2 == 0)
+                store(i, 2 * h, 2 * h + 2)
+                stored.append((i, h))
+
+        for step in range(len(unit_counts)):
+            settled = len(w1_emptied_count) // 2
+            last = step == len(unit_counts) - 1
+
+            if step + 2 < B_TILES:
+                flip_x(step + 2)
+                empty_x(step + 2)
+            if 0 <= step - 4 < B_TILES:
+                flip_mu(step - 4)
+                empty_mu(step - 4)
+            if step < len(w1_tiles):
+                flip_next_w1(w1_tiles[step])
+            if 0 <= step - 3 < B_TILES:
+                floor_norm(step - 3)
+            quantise_next_w1(settled)
+            if 0 <= step - 3 < B_TILES:
+                invert_norm(step - 3)
+                round_message(step - 3)
+            if 0 <= step - 2 < B_TILES:
+                take_norm(step - 2)
+            if 0 <= step - 1 < B_TILES:
+                add_first_bias(step - 1, 0)
+                add_first_bias(step - 1, 1)
+            store_units(0)
+            empty_next_w1()
+            if step + 2 < B_TILES:
+                quantise_x(step + 2)
+            if 0 <= step - 4 < B_TILES:
+                quantise_mu(step - 4)
+            if step < B_TILES:
+                first_matmul(step)
+            for i, h in units[len(multiplied) : len(multiplied) + unit_counts[step]]:
+                for n in (2 * h, 2 * h + 1):
+                    multiply(i, n)
+                    add_second_bias(i, n)
+                    if len(multiplied) == len(units) - 1:
+                        relu(half_of(i, n), n % 2 == 0)
+                        store(i, n, n + 1)
+                if last: store_units(0)
+                multiplied.append((i, h))

@@ -97,6 +97,15 @@ def tile_modelgraphpolicy_pb_kernel(tc, xum, action, up_w3, up_b3, dyn_w1_mu, dy
         nc.vector.memset(one[:], 1.0)
         nc.scalar.sqrt(one[:], one[:])
 
+        zeros = const.tile([P, BANK], BF16)
+        nc.vector.memset(zeros[:].bitcast(I32), 0)
+
+        def keep_warm(columns):
+            unused = psum.tile([P, BANK], F32, tag="bank", name="unused")
+            nc.tensor.matmul(
+                out=unused[:, 0:columns], lhsT=zeros[:, 0:P], rhs=zeros[:, 0:columns], start=True, stop=True
+            )
+
         on_scalar = nc.scalar.copy
         on_vector = nc.vector.tensor_copy
 
@@ -288,6 +297,8 @@ def tile_modelgraphpolicy_pb_kernel(tc, xum, action, up_w3, up_b3, dyn_w1_mu, dy
             for g in range(PASSES):
                 quantise(w3_grouped[group][:, g], w3_codes[group][:, g, :], w3_scales[group][:, g, :])
 
+        for n in range(5):
+            keep_warm(BANK)
         group_of_tile = [group for group, n in enumerate(W3_GROUP_TILES) for j in range(n)]
         for j in range(W3_TILES):
             group = group_of_tile[j]
@@ -297,6 +308,8 @@ def tile_modelgraphpolicy_pb_kernel(tc, xum, action, up_w3, up_b3, dyn_w1_mu, dy
                 w3_grouped[group],
                 j - W3_GROUP_START[group],
             )
+            if j in [1,3,5]:
+                keep_warm(BANK)
             if j == 4:
                 quantise_w3(0)
             if j == 6:

@@ -30,6 +30,7 @@ GROUP = BANK // P
 W1_GROUPS = OUT // BANK
 W1_PAIRS = OUT // (2 * P)
 W3_TILES = MESSAGE // P
+MESSAGE_P = P - (K - MESSAGE) // PACK
 W3_GROUP_TILES = (4, 2, 1)
 W3_GROUP_START = (0, 4, 6)
 
@@ -53,12 +54,16 @@ def tile_modelgraphpolicy_pb_kernel(tc, xum, action, up_w3, up_b3, dyn_w1_mu, dy
         w3_rows = []
         for j in range(W3_TILES):
             tile = raw.tile([P, K], BF16, name="w3_rows%d" % j)
-            nc.sync.dma_start(out=tile[:], in_=up_w3[j * P : (j + 1) * P, :])
+            halves = PASSES if j == 0 else 1
+            for part in range(halves):
+                columns = slice(part * K // halves, (part + 1) * K // halves)
+                nc.sync.dma_start(out=tile[:, columns], in_=up_w3[j * P : (j + 1) * P, columns])
             w3_rows.append(tile)
 
         x_pairs = {}
         w1_pairs = {}
-        mu = raw.tile([P, B_TILES, K], BF16)
+        mu = raw.tile([P, B_TILES, PASSES, PAIRS, P, 2], BF16)
+        action_rows = raw.tile([P, B_TILES, K - MESSAGE], BF16)
         bias1 = const.tile([P, MESSAGE], BF16)
         bias2 = const.tile([P, OUT], BF16)
 
@@ -82,12 +87,13 @@ def tile_modelgraphpolicy_pb_kernel(tc, xum, action, up_w3, up_b3, dyn_w1_mu, dy
                 nc.sync.dma_start(out=bias1[:], in_=up_b3.partition_broadcast(P))
             if s == 1 or s == 3:
                 load_x(s // 2 + 2)
-            if s == 4:
+            if s == 2:
                 for t in range(B_TILES // 2):
                     nc.sync.dma_start(
-                        out=mu[:, 2 * t : 2 * t + 2, MESSAGE:K],
+                        out=action_rows[:, 2 * t : 2 * t + 2, :],
                         in_=action[2 * P * t : 2 * P * (t + 1), :].rearrange("(r j) a -> r j a", j=2),
                     )
+            if s == 4:
                 nc.sync.dma_start(out=bias2[:], in_=dyn_b1.partition_broadcast(P))
         out_tiles = out.rearrange("(s r j) n -> s j r n", r=P, j=2)
 
@@ -109,9 +115,9 @@ def tile_modelgraphpolicy_pb_kernel(tc, xum, action, up_w3, up_b3, dyn_w1_mu, dy
         on_scalar = nc.scalar.copy
         on_vector = nc.vector.tensor_copy
 
-        def flip(words):
+        def flip(words, order="r (g p u) -> r g u p"):
             flipped = psum.tile([P, PASSES, PAIRS, P], F32, tag="bank", name="flipped")
-            turned = words.rearrange("r (g p u) -> r g u p", g=PASSES, u=PAIRS)
+            turned = words.rearrange(order, g=PASSES, u=PAIRS)
             for g in range(PASSES):
                 for u in range(PAIRS):
                     nc.tensor.transpose(flipped[:, g, u, :], turned[:, g, u, :], identity[:])
@@ -226,20 +232,17 @@ def tile_modelgraphpolicy_pb_kernel(tc, xum, action, up_w3, up_b3, dyn_w1_mu, dy
             nc.vector.reciprocal(inverse[i][:], floored[i][:])
 
         def round_message(i):
-            if i < 6:
-                nc.gpsimd.tensor_scalar(
-                    out=mu[:, i, 0:MESSAGE],
-                    in0=z[i][:],
-                    scalar1=inverse[i][:],
-                    scalar2=0.0,
-                    op0=ALU.mult,
-                    op1=ALU.add,
+            for g, last in ((0, P), (1, MESSAGE_P)):
+                words = mu[:, i, g, :, 0:last, :]
+                values = z[i][:, g * BANK : g * BANK + last * PACK].rearrange(
+                    "b (p u e) -> b u p e", u=PAIRS, e=2
                 )
-            else:
-                nc.vector.tensor_scalar_mul(mu[:, i, 0:MESSAGE], z[i][:], inverse[i][:])
+                nc.gpsimd.tensor_scalar(
+                out=words, in0=values, scalar1=inverse[i][:], scalar2=0.0, op0=ALU.mult, op1=ALU.add
+            )
 
         def flip_mu(i):
-            mu_flipped[i] = flip(mu[:, i, :].bitcast(F32))
+            mu_flipped[i] = flip(mu[:, i].rearrange("b g u p e -> b (g u p e)").bitcast(F32), "r (g u p) -> r g u p")
 
         def empty_mu(i):
             mu_grouped[i] = new_group(1)
@@ -263,13 +266,17 @@ def tile_modelgraphpolicy_pb_kernel(tc, xum, action, up_w3, up_b3, dyn_w1_mu, dy
                     stop=(g == PASSES - 1),
                 )
 
-        def add_second_bias(i, n):
-            if n % 2 == 0:
+        def piece(i, n, first, width):
+            start = (n % 2) * BANK + first
+            return result[i, n // 2][:, start : start + width]
+
+        def add_second_bias(i, n, first, width):
+            if n % 2 == 0 and first == 0:
                 result[i, n // 2] = results.tile([P, 2 * BANK], F32, tag="result", name="result")
             nc.vector.tensor_tensor(
-                out=result[i, n // 2][:, (n % 2) * BANK : (n % 2 + 1) * BANK],
-                in0=acc[i, n][:],
-                in1=bias2[:, n * BANK : (n + 1) * BANK],
+                out=piece(i, n, first, width),
+                in0=acc[i, n][:, first : first + width],
+                in1=bias2[:, n * BANK + first : n * BANK + first + width],
                 op=ALU.add,
             )
 
@@ -281,15 +288,12 @@ def tile_modelgraphpolicy_pb_kernel(tc, xum, action, up_w3, up_b3, dyn_w1_mu, dy
             else:
                 nc.scalar.activation(out=part, in_=part, func=ACT.Relu)
 
-        def store(i, first, last):
-            start = first // 2 * 2 * BANK
+        def store(i, first, width):
+            start = first % (2 * BANK)
             nc.sync.dma_start(
-                out=out_tiles[i // 2, i % 2, :, first * BANK : last * BANK],
-                in_=result[i, first // 2][:, first * BANK - start : last * BANK - start],
+                out=out_tiles[i // 2, i % 2, :, first : first + width],
+                in_=result[i, first // (2 * BANK)][:, start : start + width],
             )
-
-        def half_of(i, n):
-            return result[i, n // 2][:, (n % 2) * BANK : (n % 2 + 1) * BANK]
 
         w3_grouped = [new_group(n) for n in W3_GROUP_TILES]
 
@@ -340,56 +344,80 @@ def tile_modelgraphpolicy_pb_kernel(tc, xum, action, up_w3, up_b3, dyn_w1_mu, dy
                 quantise_w1(len(w1_done_count))
                 w1_done_count.append(None)
 
-        w1_tiles = [2,2,2,2,1,1,2,2,2]
-        unit_counts = [0,0,0,0,0,1,1,1,1,1,2,2,2,2,2,1]
-        units = [(i, 0) for i in range(6)] + [(0, 1), (6, 0), (1, 1), (7, 0)] + [(i, 1) for i in range(2, B_TILES)]
+        w1_tiles = [2,2,2,2,2,2,2,2]
+        unit_counts = [0,0,0,0,1,1,1,1,2,2,2,2,2,2]
+        units = [(i - 3 * h, h) for i in range(B_TILES + 3) for h in range(2) if 0 <= i - 3 * h < B_TILES]
         multiplied, stored = [], []
 
-        def store_units(keep):
-            while len(stored) < len(multiplied) - keep:
-                i, h = multiplied[len(stored)]
-                for n in (2 * h, 2 * h + 1):
-                    relu(half_of(i, n), n % 2 == 0)
-                store(i, 2 * h, 2 * h + 2)
-                stored.append((i, h))
+        def store_unit(unit):
+            i, h = unit
+            for n in (2 * h, 2 * h + 1):
+                relu(piece(i, n, 0, BANK), n == 1)
+            store(i, 2 * h * BANK, 2 * BANK)
+            stored.append(unit)
 
-        for step in range(len(unit_counts)):
-            settled = len(w1_emptied_count) // 2
-            last = step == len(unit_counts) - 1
-
+        def flip_step(step):
             if step + 2 < B_TILES:
                 flip_x(step + 2)
                 empty_x(step + 2)
-            if 0 <= step - 4 < B_TILES:
-                flip_mu(step - 4)
-                empty_mu(step - 4)
+            if 0 <= step - 3 < B_TILES:
+                flip_mu(step - 3)
+                empty_mu(step - 3)
             if step < len(w1_tiles):
                 flip_next_w1(w1_tiles[step])
-            if 0 <= step - 3 < B_TILES:
-                floor_norm(step - 3)
-            quantise_next_w1(settled)
-            if 0 <= step - 3 < B_TILES:
-                invert_norm(step - 3)
-                round_message(step - 3)
-            if 0 <= step - 2 < B_TILES:
-                take_norm(step - 2)
-            if 0 <= step - 1 < B_TILES:
-                add_first_bias(step - 1, 0)
-                add_first_bias(step - 1, 1)
-            store_units(0)
-            empty_next_w1()
+
+        def quantise_step(step):
             if step + 2 < B_TILES:
                 quantise_x(step + 2)
-            if 0 <= step - 4 < B_TILES:
-                quantise_mu(step - 4)
+            if 0 <= step - 3 < B_TILES:
+                quantise_mu(step - 3)
+
+        def multiply_step(step):
             if step < B_TILES:
                 first_matmul(step)
+                add_first_bias(step, 0)
+                add_first_bias(step, 1)
             for i, h in units[len(multiplied) : len(multiplied) + unit_counts[step]]:
                 for n in (2 * h, 2 * h + 1):
                     multiply(i, n)
-                    add_second_bias(i, n)
-                    if len(multiplied) == len(units) - 1:
-                        relu(half_of(i, n), n % 2 == 0)
-                        store(i, n, n + 1)
-                if last: store_units(0)
+                    left = len(units) - len(multiplied)
+                    width = BANK // 2 if left == 1 else BANK
+                    for first in range(0, BANK, width):
+                        add_second_bias(i, n, first, width)
+                        if left <= 2:
+                            relu(piece(i, n, first, width), (n * BANK + first) // width % 2 == 0)
+                            store(i, n * BANK + first, width)
                 multiplied.append((i, h))
+                if left <= 2:
+                    stored.append((i, h))
+
+        for step in range(len(unit_counts)):
+            while False and len(stored) < len(multiplied):
+                store_unit(multiplied[len(stored)])
+            matmuls_first = False
+            settled = len(w1_emptied_count) // 2
+            if not matmuls_first:
+                flip_step(step)
+            if 0 <= step - 2 < B_TILES:
+                floor_norm(step - 2)
+            quantise_next_w1(settled)
+            if 0 <= step - 2 < B_TILES:
+                invert_norm(step - 2)
+                round_message(step - 2)
+            if 0 <= step - 1 < B_TILES:
+                take_norm(step - 1)
+            if step == 2:
+                nc.vector.tensor_copy(
+                    out=mu[:].rearrange("b i g u p e -> b i g u (p e)").bitcast(F32)[:, :, 1, :, MESSAGE_P:P],
+                    in_=action_rows[:].bitcast(F32).rearrange("b i (p u) -> b i u p", u=PAIRS),
+                )
+            while not (False) and len(stored) < len(multiplied):
+                store_unit(multiplied[len(stored)])
+            if not matmuls_first:
+                empty_next_w1()
+                quantise_step(step)
+            multiply_step(step)
+            if matmuls_first:
+                flip_step(step)
+                empty_next_w1()
+                quantise_step(step)

@@ -356,6 +356,10 @@ def tile_modelgraphpolicy_pb_kernel(tc, xum, action, up_w3, up_b3, dyn_w1_mu, dy
             store(i, 2 * h * BANK, 2 * BANK)
             stored.append(unit)
 
+        def store_units():
+            while len(stored) < len(multiplied):
+                store_unit(multiplied[len(stored)])
+
         def flip_step(step):
             if step + 2 < B_TILES:
                 flip_x(step + 2)
@@ -392,8 +396,8 @@ def tile_modelgraphpolicy_pb_kernel(tc, xum, action, up_w3, up_b3, dyn_w1_mu, dy
                     stored.append((i, h))
 
         for step in range(len(unit_counts)):
-            while False and len(stored) < len(multiplied):
-                store_unit(multiplied[len(stored)])
+            if step > B_TILES:
+                store_units()
             matmuls_first = False
             settled = len(w1_emptied_count) // 2
             if not matmuls_first:
@@ -411,12 +415,15 @@ def tile_modelgraphpolicy_pb_kernel(tc, xum, action, up_w3, up_b3, dyn_w1_mu, dy
                     out=mu[:].rearrange("b i g u p e -> b i g u (p e)").bitcast(F32)[:, :, 1, :, MESSAGE_P:P],
                     in_=action_rows[:].bitcast(F32).rearrange("b i (p u) -> b i u p", u=PAIRS),
                 )
-            while not (False) and len(stored) < len(multiplied):
-                store_unit(multiplied[len(stored)])
+            if not (step > B_TILES):
+                store_units()
             if not matmuls_first:
                 empty_next_w1()
-                quantise_step(step)
+                if not (step >= B_TILES):
+                    quantise_step(step)
             multiply_step(step)
+            if not matmuls_first and step >= B_TILES:
+                quantise_step(step)
             if matmuls_first:
                 flip_step(step)
                 empty_next_w1()

import math
from contextlib import ExitStack

import concourse.mybir as mybir
from concourse.masks import make_identity

F32 = mybir.dt.float32
BF16 = mybir.dt.bfloat16
U32 = mybir.dt.uint32
U8 = mybir.dt.uint8
I32 = mybir.dt.int32
FP8X4 = mybir.dt.float8_e4m3fn_x4
ACT = mybir.ActivationFunctionType
ALU = mybir.AluOpType

P = 128
PACK = 4
PAIRS = 2
K = 1024
PASSES = K // (P * PACK)
BANK = 512

BATCH = 1024
MESSAGE = 896
OUT = 2048
EPS = 1e-12

B_TILES = BATCH // P
GROUP = BANK // P
W1_GROUPS = OUT // BANK
W1_PAIRS = OUT // (2 * P)
W3_TILES = MESSAGE // P
MESSAGE_P = P - (K - MESSAGE) // PACK
W3_GROUP_TILES = (4, 2, 1)
W3_GROUP_START = (0, 4, 6)

FLOPS = 2 * BATCH * K * (MESSAGE + OUT)


def tile_modelgraphpolicy_pb_kernel(tc, xum, action, up_w3, up_b3, dyn_w1_mu, dyn_b1, out):
    nc = tc.nc
    with ExitStack() as ctx:
        const = ctx.enter_context(tc.tile_pool(name="const", bufs=1))
        raw = ctx.enter_context(tc.tile_pool(name="raw", bufs=1))
        operands = ctx.enter_context(tc.tile_pool(name="operands", bufs=1))
        grouped_pool = ctx.enter_context(tc.tile_pool(name="grouped", bufs=4))
        wide_pool = ctx.enter_context(tc.tile_pool(name="wide", bufs=1))
        work = ctx.enter_context(tc.tile_pool(name="work", bufs=5))
        small = ctx.enter_context(tc.tile_pool(name="small", bufs=4))
        results = ctx.enter_context(tc.tile_pool(name="results", bufs=9))
        psum = ctx.enter_context(tc.psum_pool(name="psum", bufs=8))
        ctx.enter_context(tc.manual_schedule())

        w3_rows = []
        for j in range(W3_TILES):
            tile = raw.tile([P, K], BF16, name="w3_rows%d" % j)
            halves = PASSES if j == 0 else 1
            for part in range(halves):
                columns = slice(part * K // halves, (part + 1) * K // halves)
                nc.sync.dma_start(out=tile[:, columns], in_=up_w3[j * P : (j + 1) * P, columns])
            w3_rows.append(tile)

        x_pairs = {}
        w1_pairs = {}
        mu = raw.tile([P, B_TILES, PASSES, PAIRS, P, 2], BF16)
        action_rows = raw.tile([P, B_TILES, K - MESSAGE], BF16)
        bias1 = const.tile([P, MESSAGE], BF16)
        bias2 = const.tile([P, OUT], BF16)

        def load_x(s):
            x_pairs[s] = raw.tile([P, 2, K], BF16, name="x_rows%d" % s)
            nc.sync.dma_start(
                out=x_pairs[s][:], in_=xum[2 * P * s : 2 * P * (s + 1), :].rearrange("(r j) k -> r j k", j=2)
            )

        def load_w1(s):
            w1_pairs[s] = raw.tile([P, 2, K], BF16, name="w1_rows%d" % s)
            nc.sync.dma_start(
                out=w1_pairs[s][:], in_=dyn_w1_mu[2 * P * s : 2 * P * (s + 1), :].rearrange("(j r) k -> r j k", j=2)
            )

        load_x(0)
        load_x(1)
        for s in range(W1_PAIRS):
            load_w1(s)
            if s == 0:
                nc.sync.dma_start(out=bias1[:], in_=up_b3.partition_broadcast(P))
            if s == 1 or s == 3:
                load_x(s // 2 + 2)
            if s == 2:
                for t in range(B_TILES // 2):
                    nc.sync.dma_start(
                        out=action_rows[:, 2 * t : 2 * t + 2, :],
                        in_=action[2 * P * t : 2 * P * (t + 1), :].rearrange("(r j) a -> r j a", j=2),
                    )
            if s == 4:
                nc.sync.dma_start(out=bias2[:], in_=dyn_b1.partition_broadcast(P))
        out_tiles = out.rearrange("(s r j) n -> s j r n", r=P, j=2)

        identity = const.tile([P, P], F32)
        make_identity(nc, identity[:])
        one = const.tile([P, 1], F32)
        nc.vector.memset(one[:], 1.0)
        nc.scalar.sqrt(one[:], one[:])

        zeros = const.tile([P, BANK], BF16)
        nc.vector.memset(zeros[:].bitcast(I32), 0)

        def keep_warm(columns):
            unused = psum.tile([P, BANK], F32, tag="bank", name="unused")
            nc.tensor.matmul(
                out=unused[:, 0:columns], lhsT=zeros[:, 0:P], rhs=zeros[:, 0:columns], start=True, stop=True
            )

        on_scalar = nc.scalar.copy
        on_vector = nc.vector.tensor_copy

        def flip(words, order="r (g p u) -> r g u p"):
            flipped = psum.tile([P, PASSES, PAIRS, P], F32, tag="bank", name="flipped")
            turned = words.rearrange(order, g=PASSES, u=PAIRS)
            for g in range(PASSES):
                for u in range(PAIRS):
                    nc.tensor.transpose(flipped[:, g, u, :], turned[:, g, u, :], identity[:])
            return flipped

        def new_group(tiles):
            pool = grouped_pool if tiles < GROUP else wide_pool
            return pool.tile(
                [P, PASSES, tiles * P, PACK], BF16, tag="grouped%d" % tiles, name="grouped", align_bytes=64
            )

        def empty(copy, flipped, grouped, j):
            rows = grouped[:, :, j * P : (j + 1) * P, :].rearrange("p g r t -> p g (r t)")
            copy(
                out=rows.bitcast(F32).rearrange("p g (r u) -> p g r u", u=PAIRS),
                in_=flipped[:].rearrange("p g u r -> p g r u"),
            )

        def quantise(grouped, codes, scales):
            nc.vector.quantize_mx(
                out=codes.bitcast(FP8X4), scales=scales, in_=grouped.rearrange("p c t -> p (c t)")
            )

        def quantise_stationary(grouped, codes, scales):
            nc.vector.quantize_mx(
                out=codes.rearrange("p g b -> p (g b)").bitcast(FP8X4),
                scales=scales.rearrange("p g b -> p (g b)"),
                in_=grouped[:].rearrange("p g b t -> p (g b t)"),
            )

        x_codes = operands.tile([P, B_TILES, PASSES, P], U32, align_bytes=64)
        x_scales = operands.tile([P, B_TILES, PASSES, P], U8, align_bytes=64)
        mu_codes = operands.tile([P, B_TILES, PASSES, P], U32, align_bytes=64)
        mu_scales = operands.tile([P, B_TILES, PASSES, P], U8, align_bytes=64)
        w3_codes = [
            operands.tile([P, PASSES, n * P], U32, name="w3_codes%d" % n, align_bytes=64) for n in W3_GROUP_TILES
        ]
        w3_scales = [
            operands.tile([P, PASSES, n * P], U8, name="w3_scales%d" % n, align_bytes=64) for n in W3_GROUP_TILES
        ]
        w1_codes = [
            operands.tile([P, PASSES, BANK], U32, name="w1_codes%d" % n, align_bytes=64) for n in range(W1_GROUPS)
        ]
        w1_scales = [
            operands.tile([P, PASSES, BANK], U8, name="w1_scales%d" % n, align_bytes=64) for n in range(W1_GROUPS)
        ]

        x_flipped, x_grouped, w1_flipped, w1_grouped = {}, {}, {}, {}
        z_ps, z, norm, floored, inverse, mu_flipped, mu_grouped = {}, {}, {}, {}, {}, {}, {}

        def flip_x(i):
            x_flipped[i] = flip(x_pairs[i // 2][:, i % 2, :].bitcast(F32))

        def empty_x(i):
            x_grouped[i] = new_group(1)
            empty(on_scalar, x_flipped[i], x_grouped[i], 0)

        def quantise_x(i):
            quantise_stationary(x_grouped[i], x_codes[:, i], x_scales[:, i])

        def flip_w1(j):
            w1_flipped[j] = flip(w1_pairs[j // 2][:, j % 2, :].bitcast(F32))

        def empty_w1(j, copy):
            if j % 2 == 0:
                w1_grouped[j // 2] = new_group(2)
            empty(copy, w1_flipped[j], w1_grouped[j // 2], j % 2)

        def quantise_w1(s):
            columns = slice((s % 2) * 2 * P, (s % 2 + 1) * 2 * P)
            for g in range(PASSES):
                quantise(
                    w1_grouped[s][:, g], w1_codes[s // 2][:, g, columns], w1_scales[s // 2][:, g, columns]
                )

        def first_matmul(i):
            z_ps[i] = [psum.tile([P, BANK], F32, tag="bank", name="z_ps%d" % h) for h in range(2)]
            for codes, scales, first, tiles in zip(w3_codes, w3_scales, W3_GROUP_START, W3_GROUP_TILES):
                start, width = first * P, tiles * P
                for g in range(PASSES):
                    nc.tensor.matmul_mx(
                        out=z_ps[i][start // BANK][:, start % BANK : start % BANK + width],
                        lhsT=x_codes[:, i, g, :].bitcast(FP8X4),
                        lhsT_scale=x_scales[:, i, g, :],
                        rhs=codes[:, g, :].bitcast(FP8X4),
                        rhs_scale=scales[:, g, :],
                        start=(g == 0),
                        stop=(g == PASSES - 1),
                    )

        def add_first_bias(i, h):
            first, last = h * BANK, min((h + 1) * BANK, MESSAGE)
            if h == 0:
                z[i] = work.tile([P, MESSAGE], F32, tag="z", name="z")
            nc.vector.tensor_tensor(
                out=z[i][:, first:last], in0=z_ps[i][h][:, 0 : last - first], in1=bias1[:, first:last], op=ALU.add
            )

        def take_norm(i):
            squares = wide_pool.tile([P, MESSAGE], F32, tag="squares", name="squares")
            sum_squares = small.tile([P, 1], F32, tag="sum_squares", name="sum_squares")
            nc.scalar.activation(out=squares[:], in_=z[i][:], func=ACT.Square, accum_out=sum_squares[:])
            norm[i] = small.tile([P, 1], F32, tag="norm", name="norm")
            nc.scalar.sqrt(norm[i][:], sum_squares[:])

        def floor_norm(i):
            floored[i] = small.tile([P, 1], F32, tag="floored", name="floored")
            nc.vector.tensor_scalar_max(floored[i][:], norm[i][:], EPS)

        def invert_norm(i):
            inverse[i] = small.tile([P, 1], F32, tag="inverse", name="inverse")
            nc.vector.reciprocal(inverse[i][:], floored[i][:])

        def round_message(i):
            for g, last in ((0, P), (1, MESSAGE_P)):
                words = mu[:, i, g, :, 0:last, :]
                values = z[i][:, g * BANK : g * BANK + last * PACK].rearrange(
                    "b (p u e) -> b u p e", u=PAIRS, e=2
                )
                nc.gpsimd.tensor_scalar(
                out=words, in0=values, scalar1=inverse[i][:], scalar2=0.0, op0=ALU.mult, op1=ALU.add
            )

        def flip_mu(i):
            mu_flipped[i] = flip(mu[:, i].rearrange("b g u p e -> b (g u p e)").bitcast(F32), "r (g u p) -> r g u p")

        def empty_mu(i):
            mu_grouped[i] = new_group(1)
            empty(on_scalar, mu_flipped[i], mu_grouped[i], 0)

        def quantise_mu(i):
            quantise_stationary(mu_grouped[i], mu_codes[:, i], mu_scales[:, i])

        result, acc = {}, {}

        def multiply(i, n):
            acc[i, n] = psum.tile([P, BANK], F32, tag="bank", name="acc")
            for g in range(PASSES):
                nc.tensor.matmul_mx(
                    out=acc[i, n][:],
                    lhsT=mu_codes[:, i, g, :].bitcast(FP8X4),
                    lhsT_scale=mu_scales[:, i, g, :],
                    rhs=w1_codes[n][:, g, :].bitcast(FP8X4),
                    rhs_scale=w1_scales[n][:, g, :],
                    start=(g == 0),
                    stop=(g == PASSES - 1),
                )

        def piece(i, n, first, width):
            start = (n % 2) * BANK + first
            return result[i, n // 2][:, start : start + width]

        def add_second_bias(i, n, first, width):
            if n % 2 == 0 and first == 0:
                result[i, n // 2] = results.tile([P, 2 * BANK], F32, tag="result", name="result")
            nc.vector.tensor_tensor(
                out=piece(i, n, first, width),
                in0=acc[i, n][:, first : first + width],
                in1=bias2[:, n * BANK + first : n * BANK + first + width],
                op=ALU.add,
            )

        def relu(part, on_gpsimd):
            if on_gpsimd:
                nc.gpsimd.tensor_scalar(
                    out=part, in0=part, scalar1=math.inf, scalar2=0.0, op0=ALU.min, op1=ALU.max
                )
            else:
                nc.scalar.activation(out=part, in_=part, func=ACT.Relu)

        def store(i, first, width):
            start = first % (2 * BANK)
            nc.sync.dma_start(
                out=out_tiles[i // 2, i % 2, :, first : first + width],
                in_=result[i, first // (2 * BANK)][:, start : start + width],
            )

        w3_grouped = [new_group(n) for n in W3_GROUP_TILES]

        def quantise_w3(group):
            for g in range(PASSES):
                quantise(w3_grouped[group][:, g], w3_codes[group][:, g, :], w3_scales[group][:, g, :])

        for n in range(5):
            keep_warm(BANK)
        group_of_tile = [group for group, n in enumerate(W3_GROUP_TILES) for j in range(n)]
        for j in range(W3_TILES):
            group = group_of_tile[j]
            empty(
                on_vector if j % 2 == 1 else on_scalar,
                flip(w3_rows[j][:].bitcast(F32)),
                w3_grouped[group],
                j - W3_GROUP_START[group],
            )
            if j in [1,3,5]:
                keep_warm(BANK)
            if j == 4:
                quantise_w3(0)
            if j == 6:
                quantise_w3(1)
        flip_x(0)
        empty_x(0)
        quantise_w3(2)
        flip_x(1)
        empty_x(1)
        quantise_x(0)
        quantise_x(1)

        w1_flipped_count, w1_emptied_count, w1_done_count = [], [], []

        def flip_next_w1(count):
            for n in range(count):
                flip_w1(len(w1_flipped_count))
                w1_flipped_count.append(None)

        def empty_next_w1():
            while len(w1_emptied_count) < len(w1_flipped_count):
                j = len(w1_emptied_count)
                empty_w1(j, on_vector if False else on_scalar)
                w1_emptied_count.append(None)

        def quantise_next_w1(pairs):
            while len(w1_done_count) < pairs:
                quantise_w1(len(w1_done_count))
                w1_done_count.append(None)

        w1_tiles = [2,2,2,2,2,2,2,2]
        unit_counts = [0,0,0,0,1,1,1,1,2,2,2,2,2,2]
        units = [(i - 3 * h, h) for i in range(B_TILES + 3) for h in range(2) if 0 <= i - 3 * h < B_TILES]
        multiplied, stored = [], []

        def store_unit(unit):
            i, h = unit
            for n in (2 * h, 2 * h + 1):
                relu(piece(i, n, 0, BANK), n == 1)
            store(i, 2 * h * BANK, 2 * BANK)
            stored.append(unit)

        def store_units():
            while len(stored) < len(multiplied):
                store_unit(multiplied[len(stored)])

        def flip_step(step):
            if step + 2 < B_TILES:
                flip_x(step + 2)
                empty_x(step + 2)
            if 0 <= step - 3 < B_TILES:
                flip_mu(step - 3)
                empty_mu(step - 3)
            if step < len(w1_tiles):
                flip_next_w1(w1_tiles[step])

        def quantise_step(step):
            if step + 2 < B_TILES:
                quantise_x(step + 2)
            if 0 <= step - 3 < B_TILES:
                quantise_mu(step - 3)

        def multiply_step(step):
            if step < B_TILES:
                first_matmul(step)
                add_first_bias(step, 0)
                add_first_bias(step, 1)
            for i, h in units[len(multiplied) : len(multiplied) + unit_counts[step]]:
                for n in (2 * h, 2 * h + 1):
                    multiply(i, n)
                    left = len(units) - len(multiplied)
                    width = BANK // 2 if left == 1 else BANK
                    for first in range(0, BANK, width):
                        add_second_bias(i, n, first, width)
                        if left <= 2:
                            relu(piece(i, n, first, width), (n * BANK + first) // width % 2 == 0)
                            store(i, n * BANK + first, width)
                multiplied.append((i, h))
                if left <= 2:
                    stored.append((i, h))

        for step in range(len(unit_counts)):
            if step > B_TILES:
                store_units()
            matmuls_first = False
            settled = len(w1_emptied_count) // 2
            if not matmuls_first:
                flip_step(step)
            if 0 <= step - 2 < B_TILES:
                floor_norm(step - 2)
            quantise_next_w1(settled)
            if 0 <= step - 2 < B_TILES:
                invert_norm(step - 2)
                round_message(step - 2)
            if 0 <= step - 1 < B_TILES:
                take_norm(step - 1)
            if step == 2:
                nc.vector.tensor_copy(
                    out=mu[:].rearrange("b i g u p e -> b i g u (p e)").bitcast(F32)[:, :, 1, :, MESSAGE_P:P],
                    in_=action_rows[:].bitcast(F32).rearrange("b i (p u) -> b i u p", u=PAIRS),
                )
            if not (step > B_TILES):
                store_units()
            if not matmuls_first:
                empty_next_w1()
                if not (step >= B_TILES):
                    quantise_step(step)
            multiply_step(step)
            if not matmuls_first and step >= B_TILES:
                quantise_step(step)
            if matmuls_first:
                flip_step(step)
                empty_next_w1()
                quantise_step(step)
